import numpy as np
import ml_dtypes


def mxq(x, axis, fmt="e4m3"):
    dtype, down = {"e4m3": (ml_dtypes.float8_e4m3fn, 7), "e5m2": (ml_dtypes.float8_e5m2, 14)}[fmt]
    v = np.moveaxis(np.asarray(x, np.float32).astype(ml_dtypes.bfloat16).astype(np.float64), axis, -1)
    blocks = v.reshape(v.shape[:-1] + (-1, 32))
    amax = np.abs(blocks).max(-1, keepdims=True)
    byte = np.maximum(np.where(amax > 0, np.frexp(amax)[1] - 1 + 127, 0) - down, 1)
    scale = np.exp2(byte - 127.0)
    codes = (blocks / scale).astype(np.float32).astype(dtype).astype(np.float64)
    return np.moveaxis((codes * scale).reshape(v.shape), -1, axis)


WIDE = False


def mx_kscale(k):
    if not WIDE:
        return np.ones(k)
    levels = np.array([10, -10, 5, -5, 0])
    a = np.random.permutation(np.resize(levels, k // 512 * 4)).reshape(k // 512, 4)
    idx = np.arange(k)
    return np.exp2(a[idx // 512, idx % 128 // 32])


BF16 = ml_dtypes.bfloat16


def bf(x):
    return np.asarray(x, np.float32).astype(BF16)


def f64(x):
    return np.asarray(x).astype(np.float64)


B, D, H, L, M = 2048, 768, 1024, 512, 512
LN_EPS = 1e-5


def layer_norm(v, g, b):
    m = v.mean(-1, keepdims=True)
    var = np.square(v - m).mean(-1, keepdims=True)
    return (v - m) / np.sqrt(var + LN_EPS) * g + b


def lrelu(v):
    return np.where(v >= 0.0, v, 0.2 * v)


def setup_inputs():
    s = mx_kscale(H)
    return {
        "h1": bf(lrelu(np.random.standard_normal((B, H))) * s),
        "eps": bf(np.random.standard_normal((B, L))),
        "enc_w2": bf(np.random.standard_normal((H, H)) * 0.7 / np.sqrt(H) / s[None, :]),
        "enc_b2": bf(np.random.standard_normal(H) * 0.1),
        "ln2_g": bf(1.0 + np.random.standard_normal(H) * 0.1),
        "ln2_b": bf(np.random.standard_normal(H) * 0.1),
        "mu_w": bf(np.random.standard_normal((L, H)) * 0.7 / np.sqrt(H)),
        "mu_b": bf(np.random.standard_normal(L) * 0.1),
        "lv_w": bf(np.random.standard_normal((L, H)) * 0.7 / np.sqrt(H)),
        "lv_b": bf(np.random.standard_normal(L) * 0.1),
    }


def reference(h1, eps, enc_w2, enc_b2, ln2_g, ln2_b, mu_w, mu_b, lv_w, lv_b):
    a = (mxq(f64(h1), 1, "e4m3") @ mxq(f64(enc_w2), 1, "e4m3").T) + f64(enc_b2)
    h = lrelu(layer_norm(a, f64(ln2_g), f64(ln2_b)))
    hq = mxq(h, 1, "e4m3")
    mu = (hq @ mxq(f64(mu_w), 1, "e4m3").T) + f64(mu_b)
    logvar = (hq @ mxq(f64(lv_w), 1, "e4m3").T) + f64(lv_b)
    z = mu + f64(eps) * np.exp(0.5 * logvar)
    return mu, logvar, z

@@ -1,0 +1,392 @@
+from contextlib import ExitStack
+
+import concourse.mybir as mybir
+from concourse.masks import make_identity
+
+F32 = mybir.dt.float32
+BF16 = mybir.dt.bfloat16
+U32 = mybir.dt.uint32
+U8 = mybir.dt.uint8
+FP8X4 = mybir.dt.float8_e4m3fn_x4
+ALU = mybir.AluOpType
+ACT = mybir.ActivationFunctionType
+
+B, H, L = 2048, 1024, 512
+LN_EPS = 1e-5
+SLOPE = 0.2
+
+P = 128
+PACK = 4
+PAIR = 2
+HALVES = PACK // PAIR
+K_PASS = P * PACK
+PASSES = H // K_PASS
+N_TILE = 512
+BLOCKS = H // P
+TILES = B // P
+GROUP_TILES = 4
+GROUP_ROWS = GROUP_TILES * P
+GROUPS = TILES // GROUP_TILES
+BLOCKS_A_TICK = BLOCKS // GROUP_TILES
+TICKS_A_PASS = PACK // BLOCKS_A_TICK
+UNITS = 4
+EARLY_TILES = 8
+
+LAG_QUANTISE = 1
+LAG_ENCODE = 3
+LAG_VARIANCE = 5
+LAG_NORMALISE = 6
+LAG_TURN = LAG_NORMALISE + GROUP_TILES
+LAG_LRELU = LAG_TURN + 1
+LAG_REQUANTISE = LAG_TURN + 2
+LAG_HEADS = LAG_REQUANTISE + GROUP_TILES
+LAG_EXP = LAG_HEADS + 1
+LAG_Z = LAG_HEADS + 2
+
+FLOPS = 2 * B * H * H + 2 * 2 * B * H * L
+
+
+def tile_enhancedmlpdenoisingvae_pa_kernel(
+    tc, h1, eps, enc_w2, enc_b2, ln2_g, ln2_b, mu_w, mu_b, lv_w, lv_b, out_0, out_1, out_2
+):
+    nc = tc.nc
+    with ExitStack() as stack:
+        stack.enter_context(tc.manual_schedule())
+        consts = stack.enter_context(tc.tile_pool(name="consts", bufs=1))
+        raw = stack.enter_context(tc.tile_pool(name="raw", bufs=4))
+        rows = stack.enter_context(tc.tile_pool(name="rows", bufs=4))
+        junk = stack.enter_context(tc.tile_pool(name="junk", bufs=2))
+        encoded = stack.enter_context(tc.tile_pool(name="encoded", bufs=8))
+        normed = stack.enter_context(tc.tile_pool(name="normed", bufs=2 * GROUP_TILES))
+        small = stack.enter_context(tc.tile_pool(name="small", bufs=8))
+        stage = stack.enter_context(tc.tile_pool(name="stage", bufs=2))
+        results = stack.enter_context(tc.tile_pool(name="results", bufs=3))
+        psum = stack.enter_context(tc.psum_pool(name="psum", bufs=4))
+
+        w2_rows = enc_w2.rearrange("(a q e) k -> a q e k", a=4, e=PAIR)
+        mu_rows = mu_w.rearrange("(d i r) k -> d r i k", d=2, i=2)
+        lv_rows = lv_w.rearrange("(d i r) k -> d r i k", d=2, i=2)
+        weight_sources = [w2_rows[0:2], w2_rows[2:4], mu_rows, lv_rows]
+        h1_groups = h1.rearrange("(g p t) k -> g p (t k)", p=P, t=GROUP_TILES)
+        eps_groups = eps.rearrange("(g p t) l -> g p (t l)", p=P, t=GROUP_TILES)
+        out_groups = [
+            o.rearrange("(g p t) l -> g p t l", p=P, t=GROUP_TILES) for o in (out_0, out_1, out_2)
+        ]
+
+        w_raw = {}
+        w_codes = {}
+        w_scales = {}
+        h1_raw = {}
+        noise = {}
+        h1_grouped = {}
+        h1_codes = {}
+        h1_scales = {}
+        encodings = {}
+        row_sums = {}
+        neg_means = {}
+        rstds = {}
+        offsets = {}
+        normalised = {}
+        affine = {}
+        h_grouped = {}
+        h_codes = {}
+        h_scales = {}
+        mu_logvar = {}
+        stds = {}
+
+        def load_weights(unit):
+            w_raw[unit] = raw.tile([P, 4, H], BF16, tag="raw", name="w_raw")
+            for d in range(2):
+                nc.sync.dma_start(out=w_raw[unit][:, 2 * d : 2 * d + 2, :], in_=weight_sources[unit][d])
+
+        def load_rows(g):
+            h1_raw[g] = raw.tile([P, GROUP_TILES, H], BF16, tag="raw", name="h1_raw")
+            nc.sync.dma_start(out=h1_raw[g][:].rearrange("p t k -> p (t k)"), in_=h1_groups[g])
+
+        def load_noise(g):
+            noise[g] = consts.tile([P, GROUP_TILES, L], BF16, name="noise%d" % g)
+            nc.sync.dma_start(out=noise[g][:].rearrange("p t l -> p (t l)"), in_=eps_groups[g])
+
+        def turn_k_onto_partitions(row_words, grouped_words, copy):
+            turned = psum.tile([P, PASSES * HALVES, P], F32, tag="turned")
+            for w in range(PASSES * HALVES):
+                nc.tensor.transpose(turned[:, w, :], row_words[:, w * P : (w + 1) * P], identity[:])
+            copy(out=grouped_words, in_=turned[:].rearrange("p (c u) r -> p c r u", u=HALVES))
+
+        def quantise_weights(unit):
+            w_words = w_raw[unit][:].bitcast(F32)
+            w_grouped = stage.tile([P, PASSES, N_TILE, PACK], BF16, tag="wide", align_bytes=64)
+            w_grouped_words = w_grouped[:].bitcast(F32)
+            for i in range(4):
+                turn_k_onto_partitions(
+                    w_words[:, i, :],
+                    w_grouped_words[:, :, i * P : (i + 1) * P, :],
+                    nc.vector.tensor_copy if i % 2 == 0 else nc.scalar.copy,
+                )
+            w_codes[unit] = consts.tile([P, PASSES, N_TILE], U32, name="w_codes%d" % unit, align_bytes=64)
+            w_scales[unit] = consts.tile([P, PASSES, N_TILE], U8, name="w_scales%d" % unit, align_bytes=64)
+            nc.vector.quantize_mx(
+                out=w_codes[unit][:].rearrange("p c n -> p (c n)").bitcast(FP8X4),
+                scales=w_scales[unit][:].rearrange("p c n -> p (c n)"),
+                in_=w_grouped[:].rearrange("p c n t -> p (c n t)"),
+            )
+            if unit + 2 < UNITS:
+                load_weights(unit + 2)
+
+        def turn_rows(n):
+            if not 0 <= n < TILES:
+                return
+            g, t = divmod(n, GROUP_TILES)
+            if t == 0 and 1 <= g < GROUPS - 1:
+                load_rows(g + 1)
+            if n == (GROUPS - 2) * GROUP_TILES:
+                for later in range(GROUPS):
+                    load_noise(later)
+            h1_grouped[n] = rows.tile([P, PASSES, P, PACK], BF16, tag="h1_grouped", name="h1_grouped", align_bytes=64)
+            turn_k_onto_partitions(h1_raw[g][:].bitcast(F32)[:, t, :], h1_grouped[n][:].bitcast(F32), nc.scalar.copy)
+
+        def quantise_rows(n):
+            if not 0 <= n < TILES:
+                return
+            h1_codes[n] = rows.tile([P, PASSES, P], U32, tag="h1_codes", name="h1_codes", align_bytes=64)
+            h1_scales[n] = rows.tile([P, PASSES, P], U8, tag="h1_scales", name="h1_scales", align_bytes=64)
+            nc.vector.quantize_mx(
+                out=h1_codes[n][:].rearrange("p c r -> p (c r)").bitcast(FP8X4),
+                scales=h1_scales[n][:].rearrange("p c r -> p (c r)"),
+                in_=h1_grouped[n][:].rearrange("p c r t -> p (c r t)"),
+            )
+
+        def encode(n, half):
+            if not 0 <= n < TILES:
+                return
+            if half == 0:
+                encodings[n] = encoded.tile([P, H], F32, tag="x", name="x")
+                row_sums[n] = small.tile([P, 2], F32, tag="row_sums", name="row_sums")
+            cols = slice(half * N_TILE, (half + 1) * N_TILE)
+            acc = psum.tile([P, N_TILE], F32, tag="acc")
+            for c in range(PASSES):
+                nc.tensor.matmul_mx(
+                    out=acc[:],
+                    lhsT=h1_codes[n][:, c, :].bitcast(FP8X4),
+                    lhsT_scale=h1_scales[n][:, c, :],
+                    rhs=w_codes[half][:, c, :].bitcast(FP8X4),
+                    rhs_scale=w_scales[half][:, c, :],
+                    start=(c == 0),
+                    stop=(c == PASSES - 1),
+                )
+            nc.vector.scalar_tensor_tensor(
+                out=encodings[n][:, cols],
+                in0=acc[:],
+                scalar=1.0,
+                in1=bias1[:, cols],
+                op0=ALU.mult,
+                op1=ALU.add,
+                accum_out=row_sums[n][:, half : half + 1],
+            )
+            if half == 1:
+                neg_means[n] = small.tile([P, 1], F32, tag="neg_mean", name="neg_mean")
+                nc.gpsimd.tensor_scalar(
+                    out=neg_means[n][:],
+                    in0=row_sums[n][:, 0:1],
+                    scalar1=row_sums[n][:, 1:2],
+                    scalar2=-1.0 / H,
+                    op0=ALU.add,
+                    op1=ALU.mult,
+                )
+
+        def variance(n):
+            if not 0 <= n < TILES:
+                return
+            squares = junk.tile([P, H], BF16, tag="squares")
+            sum_sq = small.tile([P, 1], F32, tag="sum_sq")
+            nc.scalar.activation(
+                out=squares[:],
+                in_=encodings[n][:],
+                func=ACT.Square,
+                bias=neg_means[n][:],
+                scale=1.0,
+                accum_out=sum_sq[:],
+            )
+            var_eps = small.tile([P, 1], F32, tag="var_eps")
+            nc.gpsimd.tensor_scalar(
+                out=var_eps[:], in0=sum_sq[:], scalar1=1.0 / H, scalar2=LN_EPS, op0=ALU.mult, op1=ALU.add
+            )
+            rstds[n] = small.tile([P, 1], F32, tag="rstd", name="rstd")
+            nc.gpsimd.tensor_tensor(out=rstds[n][:], in0=var_eps[:], in1=neg_half[:], op=ALU.pow)
+            if n >= EARLY_TILES:
+                offsets[n] = small.tile([P, 1], F32, tag="offset", name="offset")
+                nc.gpsimd.tensor_tensor(out=offsets[n][:], in0=neg_means[n][:], in1=rstds[n][:], op=ALU.mult)
+
+        def normalise(n):
+            if not 0 <= n < TILES:
+                return
+            normalised[n] = normed.tile([P, H], F32, tag="y", name="y")
+            if n < EARLY_TILES:
+                nc.vector.tensor_scalar(
+                    out=normalised[n][:],
+                    in0=encodings[n][:],
+                    scalar1=neg_means[n][:],
+                    scalar2=rstds[n][:],
+                    op0=ALU.add,
+                    op1=ALU.mult,
+                )
+            else:
+                nc.scalar.activation(
+                    out=normalised[n][:],
+                    in_=encodings[n][:],
+                    func=ACT.Identity,
+                    bias=offsets[n][:],
+                    scale=rstds[n][:],
+                )
+
+        def turn_hidden(m):
+            if not 0 <= m < TILES:
+                return
+            g, part = divmod(m, GROUP_TILES)
+            for j in range(part * BLOCKS_A_TICK, (part + 1) * BLOCKS_A_TICK):
+                c, t = divmod(j, PACK)
+                if t == 0:
+                    affine[g, c] = stage.tile([P, PACK, GROUP_ROWS], F32, tag="wide", name="affine", align_bytes=64)
+                turned_y = psum.tile([P, GROUP_ROWS], F32, tag="turned")
+                for i in range(GROUP_TILES):
+                    nc.tensor.transpose(
+                        turned_y[:, i * P : (i + 1) * P],
+                        normalised[g * GROUP_TILES + i][:, j * P : (j + 1) * P],
+                        identity[:],
+                    )
+                nc.scalar.activation(
+                    out=affine[g, c][:, t, :],
+                    in_=turned_y[:],
+                    func=ACT.Identity,
+                    bias=gain_shift[:, BLOCKS + j : BLOCKS + j + 1],
+                    scale=gain_shift[:, j : j + 1],
+                )
+
+        def leaky_relu(m):
+            if not 0 <= m < TILES or m % TICKS_A_PASS != TICKS_A_PASS - 1:
+                return
+            g, part = divmod(m, GROUP_TILES)
+            c = part // TICKS_A_PASS
+            h_grouped[g, c] = stage.tile([P, GROUP_ROWS, PACK], BF16, tag="h_grouped", name="h_grouped", align_bytes=64)
+            by_row = affine[g, c][:].rearrange("p t r -> p r t")
+            nc.vector.scalar_tensor_tensor(
+                out=h_grouped[g, c][:], in0=by_row, scalar=SLOPE, in1=by_row, op0=ALU.mult, op1=ALU.max
+            )
+
+        def quantise_hidden(m):
+            if not 0 <= m < TILES or m % TICKS_A_PASS != TICKS_A_PASS - 1:
+                return
+            g, part = divmod(m, GROUP_TILES)
+            c = part // TICKS_A_PASS
+            if c == 0:
+                h_codes[g] = stage.tile([P, PASSES, GROUP_ROWS], U32, tag="h_codes", name="h_codes", align_bytes=64)
+                h_scales[g] = stage.tile([P, PASSES, GROUP_ROWS], U8, tag="h_scales", name="h_scales", align_bytes=64)
+            nc.vector.quantize_mx(
+                out=h_codes[g][:, c, :].bitcast(FP8X4),
+                scales=h_scales[g][:, c, :],
+                in_=h_grouped[g, c][:].rearrange("p r t -> p (r t)"),
+            )
+
+        def heads(n):
+            if not 0 <= n < TILES:
+                return
+            g, t = divmod(n, GROUP_TILES)
+            tile_rows = slice(t * P, (t + 1) * P)
+            mu_logvar[n] = []
+            for head in range(2):
+                acc = psum.tile([P, L], F32, tag="acc")
+                for c in range(PASSES):
+                    nc.tensor.matmul_mx(
+                        out=acc[:],
+                        lhsT=h_codes[g][:, c, tile_rows].bitcast(FP8X4),
+                        lhsT_scale=h_scales[g][:, c, tile_rows],
+                        rhs=w_codes[2 + head][:, c, :].bitcast(FP8X4),
+                        rhs_scale=w_scales[2 + head][:, c, :],
+                        start=(c == 0),
+                        stop=(c == PASSES - 1),
+                    )
+                result = results.tile([P, L], F32, tag="head%d" % head)
+                nc.vector.tensor_tensor(
+                    out=result[:], in0=acc[:], in1=bias2[:, head * L : (head + 1) * L], op=ALU.add
+                )
+                nc.sync.dma_start(out=out_groups[head][g][:, t, :], in_=result[:])
+                mu_logvar[n].append(result)
+
+        def exponent(n):
+            if not 0 <= n < TILES:
+                return
+            stds[n] = results.tile([P, L], F32, tag="z", name="z")
+            nc.scalar.activation(out=stds[n][:], in_=mu_logvar[n][1][:], func=ACT.Exp, scale=0.5)
+
+        def reparameterise(n):
+            if not 0 <= n < TILES:
+                return
+            g, t = divmod(n, GROUP_TILES)
+            z = stds[n]
+            nc.vector.tensor_tensor(out=z[:], in0=z[:], in1=noise[g][:, t, :], op=ALU.mult)
+            nc.vector.tensor_tensor(out=z[:], in0=z[:], in1=mu_logvar[n][0][:], op=ALU.add)
+            nc.sync.dma_start(out=out_groups[2][g][:, t, :], in_=z[:])
+
+        identity = consts.tile([P, P], F32)
+        make_identity(nc, identity[:])
+        ones = consts.tile([P, P], BF16)
+        nc.vector.memset(ones[:], 1.0)
+        neg_half = consts.tile([P, 1], F32)
+        nc.vector.memset(neg_half[:], -0.5)
+        warm = consts.tile([P, 1], F32)
+        nc.scalar.activation(out=warm[:], in_=neg_half[:], func=ACT.Exp)
+        bias_rows = consts.tile([P, H + 2 * L], BF16)
+        nc.vector.memset(bias_rows[:], 0.0)
+        nc.scalar.dma_start(out=bias_rows[0:1, 0:H], in_=enc_b2.unsqueeze(0))
+        nc.scalar.dma_start(out=bias_rows[0:1, H : H + L], in_=mu_b.unsqueeze(0))
+        nc.scalar.dma_start(out=bias_rows[0:1, H + L : H + 2 * L], in_=lv_b.unsqueeze(0))
+        gain_rows = consts.tile([P, PAIR * P], BF16)
+        nc.vector.memset(gain_rows[:], 0.0)
+        nc.scalar.dma_start(out=gain_rows[0:4, :], in_=ln2_g.rearrange("(a q) -> a q", a=4))
+        nc.scalar.dma_start(out=gain_rows[4:8, :], in_=ln2_b.rearrange("(a q) -> a q", a=4))
+
+        load_weights(0)
+        load_rows(0)
+        load_weights(1)
+        load_rows(1)
+        quantise_weights(0)
+
+        bias1 = consts.tile([P, H], F32)
+        bias2 = consts.tile([P, 2 * L], F32)
+        for i in range(2):
+            spread = psum.tile([P, N_TILE], F32, tag="acc")
+            nc.tensor.matmul(
+                out=spread[:], lhsT=ones[:], rhs=bias_rows[:, i * N_TILE : (i + 1) * N_TILE], start=True, stop=True
+            )
+            nc.scalar.copy(
+                out=bias1[:, i * N_TILE : (i + 1) * N_TILE].rearrange("p (u e q) -> p u e q", u=2, e=PAIR),
+                in_=spread[:].rearrange("p (u q e) -> p u e q", u=2, e=PAIR),
+            )
+        for i in range(2):
+            spread = psum.tile([P, N_TILE], F32, tag="acc")
+            nc.tensor.matmul(
+                out=spread[:], lhsT=ones[:], rhs=bias_rows[:, H + i * L : H + (i + 1) * L], start=True, stop=True
+            )
+            nc.scalar.copy(out=bias2[:, i * L : (i + 1) * L], in_=spread[:])
+        turned_gain = psum.tile([P, PASSES * HALVES, P], F32, tag="turned")
+        nc.tensor.transpose(turned_gain[:, 0, :], gain_rows[:].bitcast(F32), identity[:])
+        gain_words = consts.tile([P, BLOCKS], F32)
+        nc.vector.tensor_copy(out=gain_words[:], in_=turned_gain[:, 0, 0:BLOCKS])
+        gain_shift = consts.tile([P, 2 * BLOCKS], F32)
+        nc.vector.tensor_copy(out=gain_shift[:], in_=gain_words[:].bitcast(BF16))
+
+        for k in range(TILES + LAG_Z):
+            reparameterise(k - LAG_Z)
+            heads(k - LAG_HEADS)
+            exponent(k - LAG_EXP)
+            quantise_hidden(k - LAG_REQUANTISE)
+            leaky_relu(k - LAG_LRELU)
+            turn_hidden(k - LAG_TURN)
+            normalise(k - LAG_NORMALISE)
+            variance(k - LAG_VARIANCE)
+            encode(k - LAG_ENCODE - 1, 1)
+            encode(k - LAG_ENCODE, 0)
+            quantise_rows(k - LAG_QUANTISE)
+            turn_rows(k)
+            if k % 2 == 0 and 1 <= k // 2 < UNITS:
+                quantise_weights(k // 2)

@@ -18,6 +18,7 @@ SLOPE = 0.2
 P = 128
 PACK = 4
 PAIR = 2
+LINE = 4
 HALVES = PACK // PAIR
 K_PASS = P * PACK
 PASSES = H // K_PASS
@@ -67,7 +68,7 @@ def tile_enhancedmlpdenoisingvae_pa_kernel(
         mu_rows = mu_w.rearrange("(d i r) k -> d r i k", d=2, i=2)
         lv_rows = lv_w.rearrange("(d i r) k -> d r i k", d=2, i=2)
         weight_sources = [w2_rows[0:2], w2_rows[2:4], mu_rows, lv_rows]
-        h1_groups = h1.rearrange("(g p t) k -> g p (t k)", p=P, t=GROUP_TILES)
+        h1_groups = h1.rearrange("(g t p) k -> g p t k", p=P, t=GROUP_TILES)
         eps_groups = eps.rearrange("(g p t) l -> g p (t l)", p=P, t=GROUP_TILES)
         out_groups = [
             o.rearrange("(g p t) l -> g p t l", p=P, t=GROUP_TILES) for o in (out_0, out_1, out_2)
@@ -101,7 +102,7 @@ def tile_enhancedmlpdenoisingvae_pa_kernel(
 
         def load_rows(g):
             h1_raw[g] = raw.tile([P, GROUP_TILES, H], BF16, tag="raw", name="h1_raw")
-            nc.sync.dma_start(out=h1_raw[g][:].rearrange("p t k -> p (t k)"), in_=h1_groups[g])
+            nc.sync.dma_start(out=h1_raw[g][:], in_=h1_groups[g])
 
         def load_noise(g):
             noise[g] = consts.tile([P, GROUP_TILES, L], BF16, name="noise%d" % g)
@@ -246,7 +247,7 @@ def tile_enhancedmlpdenoisingvae_pa_kernel(
             for j in range(part * BLOCKS_A_TICK, (part + 1) * BLOCKS_A_TICK):
                 c, t = divmod(j, PACK)
                 if t == 0:
-                    affine[g, c] = stage.tile([P, PACK, GROUP_ROWS], F32, tag="wide", name="affine", align_bytes=64)
+                    affine[g, c] = stage.tile([P, GROUP_ROWS // LINE, PACK, LINE], F32, tag="wide", name="affine", align_bytes=64)
                 turned_y = psum.tile([P, GROUP_ROWS], F32, tag="turned")
                 for i in range(GROUP_TILES):
                     nc.tensor.transpose(
@@ -255,8 +256,8 @@ def tile_enhancedmlpdenoisingvae_pa_kernel(
                         identity[:],
                     )
                 nc.scalar.activation(
-                    out=affine[g, c][:, t, :],
-                    in_=turned_y[:],
+                    out=affine[g, c][:, :, t, :],
+                    in_=turned_y[:].rearrange("p (a i) -> p a i", i=LINE),
                     func=ACT.Identity,
                     bias=gain_shift[:, BLOCKS + j : BLOCKS + j + 1],
                     scale=gain_shift[:, j : j + 1],
@@ -267,10 +268,15 @@ def tile_enhancedmlpdenoisingvae_pa_kernel(
                 return
             g, part = divmod(m, GROUP_TILES)
             c = part // TICKS_A_PASS
-            h_grouped[g, c] = stage.tile([P, GROUP_ROWS, PACK], BF16, tag="h_grouped", name="h_grouped", align_bytes=64)
-            by_row = affine[g, c][:].rearrange("p t r -> p r t")
+            h_grouped[g, c] = stage.tile([P, GROUP_ROWS * PACK], BF16, tag="h_grouped", name="h_grouped", align_bytes=64)
+            as_it_lies = affine[g, c][:].rearrange("p a t i -> p (a t) i")
             nc.vector.scalar_tensor_tensor(
-                out=h_grouped[g, c][:], in0=by_row, scalar=SLOPE, in1=by_row, op0=ALU.mult, op1=ALU.max
+                out=h_grouped[g, c][:].rearrange("p (i m) -> p m i", i=LINE),
+                in0=as_it_lies,
+                scalar=SLOPE,
+                in1=as_it_lies,
+                op0=ALU.mult,
+                op1=ALU.max,
             )
 
         def quantise_hidden(m):
@@ -284,7 +290,7 @@ def tile_enhancedmlpdenoisingvae_pa_kernel(
             nc.vector.quantize_mx(
                 out=h_codes[g][:, c, :].bitcast(FP8X4),
                 scales=h_scales[g][:, c, :],
-                in_=h_grouped[g, c][:].rearrange("p r t -> p (r t)"),
+                in_=h_grouped[g, c][:],
             )
 
         def heads(n):

@@ -25,24 +25,19 @@ PASSES = H // K_PASS
 N_TILE = 512
 BLOCKS = H // P
 TILES = B // P
-GROUP_TILES = 4
-GROUP_ROWS = GROUP_TILES * P
-GROUPS = TILES // GROUP_TILES
-BLOCKS_A_TICK = BLOCKS // GROUP_TILES
-TICKS_A_PASS = PACK // BLOCKS_A_TICK
+PAIR_TILES = 2
+PAIRS = TILES // PAIR_TILES
 UNITS = 4
-EARLY_TILES = 8
+UNIT_TICK = {1: 0, 2: 2, 3: 3}
+BIAS_TICK = 4
+EARLY_TILES = 3
 
-LAG_QUANTISE = 1
-LAG_ENCODE = 3
-LAG_VARIANCE = 5
-LAG_NORMALISE = 6
-LAG_TURN = LAG_NORMALISE + GROUP_TILES
-LAG_LRELU = LAG_TURN + 1
-LAG_REQUANTISE = LAG_TURN + 2
-LAG_HEADS = LAG_REQUANTISE + GROUP_TILES
-LAG_EXP = LAG_HEADS + 1
-LAG_Z = LAG_HEADS + 2
+LAG_ENCODE = 1
+LAG_NORMALISE = 2
+LAG_TURN = 3
+LAG_REQUANTISE = 4
+LAG_HEADS = 5
+LAG_Z = 6
 
 FLOPS = 2 * B * H * H + 2 * 2 * B * H * L
 
@@ -54,31 +49,30 @@ def tile_enhancedmlpdenoisingvae_pa_kernel(
     with ExitStack() as stack:
         stack.enter_context(tc.manual_schedule())
         consts = stack.enter_context(tc.tile_pool(name="consts", bufs=1))
-        raw = stack.enter_context(tc.tile_pool(name="raw", bufs=4))
+        raw = stack.enter_context(tc.tile_pool(name="raw", bufs=PAIRS))
         rows = stack.enter_context(tc.tile_pool(name="rows", bufs=4))
         junk = stack.enter_context(tc.tile_pool(name="junk", bufs=2))
-        encoded = stack.enter_context(tc.tile_pool(name="encoded", bufs=8))
-        normed = stack.enter_context(tc.tile_pool(name="normed", bufs=2 * GROUP_TILES))
+        encoded = stack.enter_context(tc.tile_pool(name="encoded", bufs=4))
+        normed = stack.enter_context(tc.tile_pool(name="normed", bufs=3 * PAIR_TILES))
         small = stack.enter_context(tc.tile_pool(name="small", bufs=8))
-        stage = stack.enter_context(tc.tile_pool(name="stage", bufs=2))
-        results = stack.enter_context(tc.tile_pool(name="results", bufs=3))
+        stage = stack.enter_context(tc.tile_pool(name="stage", bufs=4))
+        results = stack.enter_context(tc.tile_pool(name="results", bufs=4))
         psum = stack.enter_context(tc.psum_pool(name="psum", bufs=4))
 
         w2_rows = enc_w2.rearrange("(a q e) k -> a q e k", a=4, e=PAIR)
         mu_rows = mu_w.rearrange("(d i r) k -> d r i k", d=2, i=2)
         lv_rows = lv_w.rearrange("(d i r) k -> d r i k", d=2, i=2)
         weight_sources = [w2_rows[0:2], w2_rows[2:4], mu_rows, lv_rows]
-        h1_groups = h1.rearrange("(g t p) k -> g p t k", p=P, t=GROUP_TILES)
-        eps_groups = eps.rearrange("(g p t) l -> g p (t l)", p=P, t=GROUP_TILES)
+        h1_groups = h1.rearrange("(g p t) k -> g p (t k)", p=P, t=PAIR_TILES)
+        eps_rows = eps.rearrange("(g p t) l -> p g (t l)", p=P, t=PAIR_TILES)
         out_groups = [
-            o.rearrange("(g p t) l -> g p t l", p=P, t=GROUP_TILES) for o in (out_0, out_1, out_2)
+            o.rearrange("(g p t) l -> g p t l", p=P, t=PAIR_TILES) for o in (out_0, out_1, out_2)
         ]
 
         w_raw = {}
         w_codes = {}
         w_scales = {}
         h1_raw = {}
-        noise = {}
         h1_grouped = {}
         h1_codes = {}
         h1_scales = {}
@@ -96,17 +90,19 @@ def tile_enhancedmlpdenoisingvae_pa_kernel(
         stds = {}
 
         def load_weights(unit):
-            w_raw[unit] = raw.tile([P, 4, H], BF16, tag="raw", name="w_raw")
+            w_raw[unit] = consts.tile([P, 4, H], BF16, name="w_raw%d" % unit)
             for d in range(2):
                 nc.sync.dma_start(out=w_raw[unit][:, 2 * d : 2 * d + 2, :], in_=weight_sources[unit][d])
 
         def load_rows(g):
-            h1_raw[g] = raw.tile([P, GROUP_TILES, H], BF16, tag="raw", name="h1_raw")
-            nc.sync.dma_start(out=h1_raw[g][:], in_=h1_groups[g])
+            h1_raw[g] = raw.tile([P, PAIR_TILES, H], BF16, tag="h1_raw", name="h1_raw")
+            nc.sync.dma_start(out=h1_raw[g][:].rearrange("p t k -> p (t k)"), in_=h1_groups[g])
 
-        def load_noise(g):
-            noise[g] = consts.tile([P, GROUP_TILES, L], BF16, name="noise%d" % g)
-            nc.sync.dma_start(out=noise[g][:].rearrange("p t l -> p (t l)"), in_=eps_groups[g])
+        def load_noise(quarter):
+            groups = slice(quarter * 2, quarter * 2 + 2)
+            nc.sync.dma_start(
+                out=noise[:, groups, :, :].rearrange("p g t l -> p g (t l)"), in_=eps_rows[:, groups, :]
+            )
 
         def turn_k_onto_partitions(row_words, grouped_words, copy):
             turned = psum.tile([P, PASSES * HALVES, P], F32, tag="turned")
@@ -116,7 +112,7 @@ def tile_enhancedmlpdenoisingvae_pa_kernel(
 
         def quantise_weights(unit):
             w_words = w_raw[unit][:].bitcast(F32)
-            w_grouped = stage.tile([P, PASSES, N_TILE, PACK], BF16, tag="wide", align_bytes=64)
+            w_grouped = consts.tile([P, PASSES, N_TILE, PACK], BF16, name="w_grouped%d" % (unit % 2), align_bytes=64)
             w_grouped_words = w_grouped[:].bitcast(F32)
             for i in range(4):
                 turn_k_onto_partitions(
@@ -131,18 +127,11 @@ def tile_enhancedmlpdenoisingvae_pa_kernel(
                 scales=w_scales[unit][:].rearrange("p c n -> p (c n)"),
                 in_=w_grouped[:].rearrange("p c n t -> p (c n t)"),
             )
-            if unit + 2 < UNITS:
-                load_weights(unit + 2)
 
         def turn_rows(n):
             if not 0 <= n < TILES:
                 return
-            g, t = divmod(n, GROUP_TILES)
-            if t == 0 and 1 <= g < GROUPS - 1:
-                load_rows(g + 1)
-            if n == (GROUPS - 2) * GROUP_TILES:
-                for later in range(GROUPS):
-                    load_noise(later)
+            g, t = divmod(n, PAIR_TILES)
             h1_grouped[n] = rows.tile([P, PASSES, P, PACK], BF16, tag="h1_grouped", name="h1_grouped", align_bytes=64)
             turn_k_onto_partitions(h1_raw[g][:].bitcast(F32)[:, t, :], h1_grouped[n][:].bitcast(F32), nc.scalar.copy)
 
@@ -240,38 +229,32 @@ def tile_enhancedmlpdenoisingvae_pa_kernel(
                     scale=rstds[n][:],
                 )
 
-        def turn_hidden(m):
-            if not 0 <= m < TILES:
+        def turn_hidden(n, c):
+            if not 0 <= n < TILES:
                 return
-            g, part = divmod(m, GROUP_TILES)
-            for j in range(part * BLOCKS_A_TICK, (part + 1) * BLOCKS_A_TICK):
-                c, t = divmod(j, PACK)
-                if t == 0:
-                    affine[g, c] = stage.tile([P, GROUP_ROWS // LINE, PACK, LINE], F32, tag="wide", name="affine", align_bytes=64)
-                turned_y = psum.tile([P, GROUP_ROWS], F32, tag="turned")
-                for i in range(GROUP_TILES):
-                    nc.tensor.transpose(
-                        turned_y[:, i * P : (i + 1) * P],
-                        normalised[g * GROUP_TILES + i][:, j * P : (j + 1) * P],
-                        identity[:],
-                    )
+            affine[n, c] = stage.tile([P, P // LINE, PACK, LINE], F32, tag="affine", name="affine", align_bytes=64)
+            turned_y = psum.tile([P, PACK, P], F32, tag="turned")
+            for t in range(PACK):
+                j = c * PACK + t
+                nc.tensor.transpose(turned_y[:, t, :], normalised[n][:, j * P : (j + 1) * P], identity[:])
+            for t in range(PACK):
+                j = c * PACK + t
                 nc.scalar.activation(
-                    out=affine[g, c][:, :, t, :],
-                    in_=turned_y[:].rearrange("p (a i) -> p a i", i=LINE),
+                    out=affine[n, c][:, :, t, :],
+                    in_=turned_y[:, t, :].rearrange("p (i a) -> p a i", i=LINE),
                     func=ACT.Identity,
                     bias=gain_shift[:, BLOCKS + j : BLOCKS + j + 1],
                     scale=gain_shift[:, j : j + 1],
                 )
 
-        def leaky_relu(m):
-            if not 0 <= m < TILES or m % TICKS_A_PASS != TICKS_A_PASS - 1:
+        def leaky_relu(n, c):
+            if not 0 <= n < TILES:
                 return
-            g, part = divmod(m, GROUP_TILES)
-            c = part // TICKS_A_PASS
-            h_grouped[g, c] = stage.tile([P, GROUP_ROWS * PACK], BF16, tag="h_grouped", name="h_grouped", align_bytes=64)
-            as_it_lies = affine[g, c][:].rearrange("p a t i -> p (a t) i")
+            if c == 0:
+                h_grouped[n] = stage.tile([P, PASSES, P * PACK], BF16, tag="h_grouped", name="h_grouped", align_bytes=64)
+            as_it_lies = affine[n, c][:].rearrange("p a t i -> p (a t) i")
             nc.vector.scalar_tensor_tensor(
-                out=h_grouped[g, c][:].rearrange("p (i m) -> p m i", i=LINE),
+                out=h_grouped[n][:, c, :].rearrange("p (i m) -> p m i", i=LINE),
                 in0=as_it_lies,
                 scalar=SLOPE,
                 in1=as_it_lies,
@@ -279,44 +262,39 @@ def tile_enhancedmlpdenoisingvae_pa_kernel(
                 op1=ALU.max,
             )
 
-        def quantise_hidden(m):
-            if not 0 <= m < TILES or m % TICKS_A_PASS != TICKS_A_PASS - 1:
-                return
-            g, part = divmod(m, GROUP_TILES)
-            c = part // TICKS_A_PASS
-            if c == 0:
-                h_codes[g] = stage.tile([P, PASSES, GROUP_ROWS], U32, tag="h_codes", name="h_codes", align_bytes=64)
-                h_scales[g] = stage.tile([P, PASSES, GROUP_ROWS], U8, tag="h_scales", name="h_scales", align_bytes=64)
-            nc.vector.quantize_mx(
-                out=h_codes[g][:, c, :].bitcast(FP8X4),
-                scales=h_scales[g][:, c, :],
-                in_=h_grouped[g, c][:],
-            )
-
-        def heads(n):
+        def quantise_hidden(n):
             if not 0 <= n < TILES:
                 return
-            g, t = divmod(n, GROUP_TILES)
-            tile_rows = slice(t * P, (t + 1) * P)
-            mu_logvar[n] = []
-            for head in range(2):
-                acc = psum.tile([P, L], F32, tag="acc")
-                for c in range(PASSES):
-                    nc.tensor.matmul_mx(
-                        out=acc[:],
-                        lhsT=h_codes[g][:, c, tile_rows].bitcast(FP8X4),
-                        lhsT_scale=h_scales[g][:, c, tile_rows],
-                        rhs=w_codes[2 + head][:, c, :].bitcast(FP8X4),
-                        rhs_scale=w_scales[2 + head][:, c, :],
-                        start=(c == 0),
-                        stop=(c == PASSES - 1),
-                    )
-                result = results.tile([P, L], F32, tag="head%d" % head)
-                nc.vector.tensor_tensor(
-                    out=result[:], in0=acc[:], in1=bias2[:, head * L : (head + 1) * L], op=ALU.add
+            h_codes[n] = stage.tile([P, PASSES, P], U32, tag="h_codes", name="h_codes", align_bytes=64)
+            h_scales[n] = stage.tile([P, PASSES, P], U8, tag="h_scales", name="h_scales", align_bytes=64)
+            nc.vector.quantize_mx(
+                out=h_codes[n][:].rearrange("p c r -> p (c r)").bitcast(FP8X4),
+                scales=h_scales[n][:].rearrange("p c r -> p (c r)"),
+                in_=h_grouped[n][:].rearrange("p c m -> p (c m)"),
+            )
+
+        def heads(n, head):
+            if not 0 <= n < TILES:
+                return
+            g, t = divmod(n, PAIR_TILES)
+            mu_logvar.setdefault(n, {})
+            acc = psum.tile([P, L], F32, tag="acc")
+            for c in range(PASSES):
+                nc.tensor.matmul_mx(
+                    out=acc[:],
+                    lhsT=h_codes[n][:, c, :].bitcast(FP8X4),
+                    lhsT_scale=h_scales[n][:, c, :],
+                    rhs=w_codes[2 + head][:, c, :].bitcast(FP8X4),
+                    rhs_scale=w_scales[2 + head][:, c, :],
+                    start=(c == 0),
+                    stop=(c == PASSES - 1),
                 )
-                nc.sync.dma_start(out=out_groups[head][g][:, t, :], in_=result[:])
-                mu_logvar[n].append(result)
+            result = results.tile([P, L], F32, tag="head%d" % head)
+            nc.vector.tensor_tensor(
+                out=result[:], in0=acc[:], in1=bias2[:, head * L : (head + 1) * L], op=ALU.add
+            )
+            nc.sync.dma_start(out=out_groups[head][g][:, t, :], in_=result[:])
+            mu_logvar[n][head] = result
 
         def exponent(n):
             if not 0 <= n < TILES:
@@ -324,12 +302,18 @@ def tile_enhancedmlpdenoisingvae_pa_kernel(
             stds[n] = results.tile([P, L], F32, tag="z", name="z")
             nc.scalar.activation(out=stds[n][:], in_=mu_logvar[n][1][:], func=ACT.Exp, scale=0.5)
 
-        def reparameterise(n):
+        def scale_noise(n):
             if not 0 <= n < TILES:
                 return
-            g, t = divmod(n, GROUP_TILES)
+            g, t = divmod(n, PAIR_TILES)
             z = stds[n]
-            nc.vector.tensor_tensor(out=z[:], in0=z[:], in1=noise[g][:, t, :], op=ALU.mult)
+            nc.vector.tensor_tensor(out=z[:], in0=z[:], in1=noise[:, g, t, :], op=ALU.mult)
+
+        def add_mu(n):
+            if not 0 <= n < TILES:
+                return
+            g, t = divmod(n, PAIR_TILES)
+            z = stds[n]
             nc.vector.tensor_tensor(out=z[:], in0=z[:], in1=mu_logvar[n][0][:], op=ALU.add)
             nc.sync.dma_start(out=out_groups[2][g][:, t, :], in_=z[:])
 
@@ -351,14 +335,22 @@ def tile_enhancedmlpdenoisingvae_pa_kernel(
         nc.scalar.dma_start(out=gain_rows[0:4, :], in_=ln2_g.rearrange("(a q) -> a q", a=4))
         nc.scalar.dma_start(out=gain_rows[4:8, :], in_=ln2_b.rearrange("(a q) -> a q", a=4))
 
+        noise = consts.tile([P, PAIRS, PAIR_TILES, L], BF16)
         load_weights(0)
         load_rows(0)
         load_weights(1)
         load_rows(1)
+        load_rows(2)
+        load_weights(2)
+        load_rows(3)
+        load_weights(3)
+        for g in range(4, PAIRS):
+            load_rows(g)
+        for quarter in range(4):
+            load_noise(quarter)
         quantise_weights(0)
 
         bias1 = consts.tile([P, H], F32)
-        bias2 = consts.tile([P, 2 * L], F32)
         for i in range(2):
             spread = psum.tile([P, N_TILE], F32, tag="acc")
             nc.tensor.matmul(
@@ -368,12 +360,6 @@ def tile_enhancedmlpdenoisingvae_pa_kernel(
                 out=bias1[:, i * N_TILE : (i + 1) * N_TILE].rearrange("p (u e q) -> p u e q", u=2, e=PAIR),
                 in_=spread[:].rearrange("p (u q e) -> p u e q", u=2, e=PAIR),
             )
-        for i in range(2):
-            spread = psum.tile([P, N_TILE], F32, tag="acc")
-            nc.tensor.matmul(
-                out=spread[:], lhsT=ones[:], rhs=bias_rows[:, H + i * L : H + (i + 1) * L], start=True, stop=True
-            )
-            nc.scalar.copy(out=bias2[:, i * L : (i + 1) * L], in_=spread[:])
         turned_gain = psum.tile([P, PASSES * HALVES, P], F32, tag="turned")
         nc.tensor.transpose(turned_gain[:, 0, :], gain_rows[:].bitcast(F32), identity[:])
         gain_words = consts.tile([P, BLOCKS], F32)
@@ -381,18 +367,35 @@ def tile_enhancedmlpdenoisingvae_pa_kernel(
         gain_shift = consts.tile([P, 2 * BLOCKS], F32)
         nc.vector.tensor_copy(out=gain_shift[:], in_=gain_words[:].bitcast(BF16))
 
+        bias2 = consts.tile([P, 2 * L], F32)
+
+        def spread_head_biases():
+            for i in range(2):
+                spread = psum.tile([P, N_TILE], F32, tag="acc")
+                nc.tensor.matmul(
+                    out=spread[:], lhsT=ones[:], rhs=bias_rows[:, H + i * L : H + (i + 1) * L], start=True, stop=True
+                )
+                nc.vector.tensor_copy(out=bias2[:, i * L : (i + 1) * L], in_=spread[:])
+
         for k in range(TILES + LAG_Z):
-            reparameterise(k - LAG_Z)
-            heads(k - LAG_HEADS)
-            exponent(k - LAG_EXP)
-            quantise_hidden(k - LAG_REQUANTISE)
-            leaky_relu(k - LAG_LRELU)
-            turn_hidden(k - LAG_TURN)
-            normalise(k - LAG_NORMALISE)
-            variance(k - LAG_VARIANCE)
-            encode(k - LAG_ENCODE - 1, 1)
-            encode(k - LAG_ENCODE, 0)
-            quantise_rows(k - LAG_QUANTISE)
+            for c in range(PASSES):
+                turn_hidden(k - LAG_TURN, c)
             turn_rows(k)
-            if k % 2 == 0 and 1 <= k // 2 < UNITS:
-                quantise_weights(k // 2)
+            for half in range(2):
+                encode(k - LAG_ENCODE, half)
+            scale_noise(k - LAG_Z)
+            for head in (1, 0):
+                heads(k - LAG_HEADS, head)
+            normalise(k - LAG_NORMALISE)
+            leaky_relu(k - LAG_TURN, 0)
+            add_mu(k - LAG_Z)
+            quantise_rows(k)
+            leaky_relu(k - LAG_TURN, 1)
+            variance(k - LAG_ENCODE)
+            exponent(k - LAG_HEADS)
+            quantise_hidden(k - LAG_REQUANTISE)
+            for unit in range(1, UNITS):
+                if k == UNIT_TICK[unit]:
+                    quantise_weights(unit)
+            if k == BIAS_TICK:
+                spread_head_biases()

@@ -28,16 +28,21 @@ TILES = B // P
 PAIR_TILES = 2
 PAIRS = TILES // PAIR_TILES
 UNITS = 4
-UNIT_TICK = {1: 0, 2: 2, 3: 3}
-BIAS_TICK = 4
-EARLY_TILES = 3
+UNIT_TICK = {1: 0, 2: 2, 3: 6}
+BIAS_TICK = 7
+EARLY_TILES = 5
 
-LAG_ENCODE = 1
-LAG_NORMALISE = 2
-LAG_TURN = 3
-LAG_REQUANTISE = 4
-LAG_HEADS = 5
-LAG_Z = 6
+LAG_QUANTISE = 1
+LAG_ENCODE = 3
+LAG_ADD_BIAS = 4
+LAG_NORMALISE = 6
+LAG_TURN = 7
+LAG_LRELU = 8
+LAG_REQUANTISE = 9
+LAG_HEADS = 10
+LAG_HEAD_BIAS = 11
+LAG_SCALE_NOISE = 12
+LAG_ADD_MU = 13
 
 FLOPS = 2 * B * H * H + 2 * 2 * B * H * L
 
@@ -52,11 +57,12 @@ def tile_enhancedmlpdenoisingvae_pa_kernel(
         raw = stack.enter_context(tc.tile_pool(name="raw", bufs=PAIRS))
         rows = stack.enter_context(tc.tile_pool(name="rows", bufs=4))
         junk = stack.enter_context(tc.tile_pool(name="junk", bufs=2))
-        encoded = stack.enter_context(tc.tile_pool(name="encoded", bufs=4))
-        normed = stack.enter_context(tc.tile_pool(name="normed", bufs=3 * PAIR_TILES))
+        encoded = stack.enter_context(tc.tile_pool(name="encoded", bufs=6))
+        normed = stack.enter_context(tc.tile_pool(name="normed", bufs=8))
         small = stack.enter_context(tc.tile_pool(name="small", bufs=8))
         stage = stack.enter_context(tc.tile_pool(name="stage", bufs=4))
         results = stack.enter_context(tc.tile_pool(name="results", bufs=4))
+        part = stack.enter_context(tc.tile_pool(name="part", bufs=1))
         psum = stack.enter_context(tc.psum_pool(name="psum", bufs=4))
 
         w2_rows = enc_w2.rearrange("(a q e) k -> a q e k", a=4, e=PAIR)
@@ -88,9 +94,10 @@ def tile_enhancedmlpdenoisingvae_pa_kernel(
         h_scales = {}
         mu_logvar = {}
         stds = {}
+        parts = {}
 
         def load_weights(unit):
-            w_raw[unit] = consts.tile([P, 4, H], BF16, name="w_raw%d" % unit)
+            w_raw[unit] = consts.tile([P, 4, H], BF16, name="w_raw%d" % (unit % 2))
             for d in range(2):
                 nc.sync.dma_start(out=w_raw[unit][:, 2 * d : 2 * d + 2, :], in_=weight_sources[unit][d])
 
@@ -104,10 +111,13 @@ def tile_enhancedmlpdenoisingvae_pa_kernel(
                 out=noise[:, groups, :, :].rearrange("p g t l -> p g (t l)"), in_=eps_rows[:, groups, :]
             )
 
-        def turn_k_onto_partitions(row_words, grouped_words, copy):
-            turned = psum.tile([P, PASSES * HALVES, P], F32, tag="turned")
+        def turn_words(row_words):
+            turned = psum.tile([P, PASSES * HALVES, P], F32, tag="turned", name="turned")
             for w in range(PASSES * HALVES):
                 nc.tensor.transpose(turned[:, w, :], row_words[:, w * P : (w + 1) * P], identity[:])
+            return turned
+
+        def lay_side_by_side(turned, grouped_words, copy):
             copy(out=grouped_words, in_=turned[:].rearrange("p (c u) r -> p c r u", u=HALVES))
 
         def quantise_weights(unit):
@@ -115,8 +125,8 @@ def tile_enhancedmlpdenoisingvae_pa_kernel(
             w_grouped = consts.tile([P, PASSES, N_TILE, PACK], BF16, name="w_grouped%d" % (unit % 2), align_bytes=64)
             w_grouped_words = w_grouped[:].bitcast(F32)
             for i in range(4):
-                turn_k_onto_partitions(
-                    w_words[:, i, :],
+                lay_side_by_side(
+                    turn_words(w_words[:, i, :]),
                     w_grouped_words[:, :, i * P : (i + 1) * P, :],
                     nc.vector.tensor_copy if i % 2 == 0 else nc.scalar.copy,
                 )
@@ -128,12 +138,19 @@ def tile_enhancedmlpdenoisingvae_pa_kernel(
                 in_=w_grouped[:].rearrange("p c n t -> p (c n t)"),
             )
 
+        turned_rows = {}
+
         def turn_rows(n):
             if not 0 <= n < TILES:
                 return
             g, t = divmod(n, PAIR_TILES)
+            turned_rows[n] = turn_words(h1_raw[g][:].bitcast(F32)[:, t, :])
+
+        def group_rows(n):
+            if not 0 <= n < TILES:
+                return
             h1_grouped[n] = rows.tile([P, PASSES, P, PACK], BF16, tag="h1_grouped", name="h1_grouped", align_bytes=64)
-            turn_k_onto_partitions(h1_raw[g][:].bitcast(F32)[:, t, :], h1_grouped[n][:].bitcast(F32), nc.scalar.copy)
+            lay_side_by_side(turned_rows[n], h1_grouped[n][:].bitcast(F32), nc.scalar.copy)
 
         def quantise_rows(n):
             if not 0 <= n < TILES:
@@ -146,14 +163,13 @@ def tile_enhancedmlpdenoisingvae_pa_kernel(
                 in_=h1_grouped[n][:].rearrange("p c r t -> p (c r t)"),
             )
 
-        def encode(n, half):
+        accs = {}
+
+        def multiply_first(n, half):
             if not 0 <= n < TILES:
                 return
-            if half == 0:
-                encodings[n] = encoded.tile([P, H], F32, tag="x", name="x")
-                row_sums[n] = small.tile([P, 2], F32, tag="row_sums", name="row_sums")
-            cols = slice(half * N_TILE, (half + 1) * N_TILE)
-            acc = psum.tile([P, N_TILE], F32, tag="acc")
+            acc = psum.tile([P, N_TILE], F32, tag="acc", name="acc")
+            accs[n, half] = acc
             for c in range(PASSES):
                 nc.tensor.matmul_mx(
                     out=acc[:],
@@ -164,29 +180,32 @@ def tile_enhancedmlpdenoisingvae_pa_kernel(
                     start=(c == 0),
                     stop=(c == PASSES - 1),
                 )
+
+        def add_first_bias(n, half):
+            if not 0 <= n < TILES:
+                return
+            if half == 0:
+                encodings[n] = encoded.tile([P, H], F32, tag="x", name="x")
+                row_sums[n] = small.tile([P, 2], F32, tag="row_sums", name="row_sums")
+            cols = slice(half * N_TILE, (half + 1) * N_TILE)
             nc.vector.scalar_tensor_tensor(
                 out=encodings[n][:, cols],
-                in0=acc[:],
+                in0=accs[n, half][:],
                 scalar=1.0,
                 in1=bias1[:, cols],
                 op0=ALU.mult,
                 op1=ALU.add,
                 accum_out=row_sums[n][:, half : half + 1],
             )
-            if half == 1:
-                neg_means[n] = small.tile([P, 1], F32, tag="neg_mean", name="neg_mean")
-                nc.gpsimd.tensor_scalar(
-                    out=neg_means[n][:],
-                    in0=row_sums[n][:, 0:1],
-                    scalar1=row_sums[n][:, 1:2],
-                    scalar2=-1.0 / H,
-                    op0=ALU.add,
-                    op1=ALU.mult,
-                )
 
         def variance(n):
             if not 0 <= n < TILES:
                 return
+            shares = small.tile([P, 2], F32, tag="shares")
+            neg_means[n] = small.tile([P, 1], F32, tag="neg_mean", name="neg_mean")
+            nc.scalar.activation(
+                out=shares[:], in_=row_sums[n][:], func=ACT.Identity, scale=-1.0 / H, accum_out=neg_means[n][:]
+            )
             squares = junk.tile([P, H], BF16, tag="squares")
             sum_sq = small.tile([P, 1], F32, tag="sum_sq")
             nc.scalar.activation(
@@ -229,19 +248,26 @@ def tile_enhancedmlpdenoisingvae_pa_kernel(
                     scale=rstds[n][:],
                 )
 
+        turned_hidden = {}
+
         def turn_hidden(n, c):
             if not 0 <= n < TILES:
                 return
-            affine[n, c] = stage.tile([P, P // LINE, PACK, LINE], F32, tag="affine", name="affine", align_bytes=64)
-            turned_y = psum.tile([P, PACK, P], F32, tag="turned")
+            turned_y = psum.tile([P, PACK, P], F32, tag="turned", name="turned")
+            turned_hidden[n, c] = turned_y
             for t in range(PACK):
                 j = c * PACK + t
                 nc.tensor.transpose(turned_y[:, t, :], normalised[n][:, j * P : (j + 1) * P], identity[:])
+
+        def gain_and_shift(n, c):
+            if not 0 <= n < TILES:
+                return
+            affine[n, c] = stage.tile([P, P // LINE, PACK, LINE], F32, tag="affine", name="affine", align_bytes=64)
             for t in range(PACK):
                 j = c * PACK + t
                 nc.scalar.activation(
                     out=affine[n, c][:, :, t, :],
-                    in_=turned_y[:, t, :].rearrange("p (i a) -> p a i", i=LINE),
+                    in_=turned_hidden[n, c][:, t, :].rearrange("p (i a) -> p a i", i=LINE),
                     func=ACT.Identity,
                     bias=gain_shift[:, BLOCKS + j : BLOCKS + j + 1],
                     scale=gain_shift[:, j : j + 1],
@@ -273,12 +299,11 @@ def tile_enhancedmlpdenoisingvae_pa_kernel(
                 in_=h_grouped[n][:].rearrange("p c m -> p (c m)"),
             )
 
-        def heads(n, head):
+        def multiply_head(n, head):
             if not 0 <= n < TILES:
                 return
-            g, t = divmod(n, PAIR_TILES)
-            mu_logvar.setdefault(n, {})
-            acc = psum.tile([P, L], F32, tag="acc")
+            acc = psum.tile([P, L], F32, tag="acc", name="acc")
+            accs[n, 2 + head] = acc
             for c in range(PASSES):
                 nc.tensor.matmul_mx(
                     out=acc[:],
@@ -289,9 +314,15 @@ def tile_enhancedmlpdenoisingvae_pa_kernel(
                     start=(c == 0),
                     stop=(c == PASSES - 1),
                 )
-            result = results.tile([P, L], F32, tag="head%d" % head)
+
+        def add_head_bias(n, head):
+            if not 0 <= n < TILES:
+                return
+            g, t = divmod(n, PAIR_TILES)
+            mu_logvar.setdefault(n, {})
+            result = results.tile([P, L], F32, tag="head%d" % head, name="head%d" % head)
             nc.vector.tensor_tensor(
-                out=result[:], in0=acc[:], in1=bias2[:, head * L : (head + 1) * L], op=ALU.add
+                out=result[:], in0=accs[n, 2 + head][:], in1=bias2[:, head * L : (head + 1) * L], op=ALU.add
             )
             nc.sync.dma_start(out=out_groups[head][g][:, t, :], in_=result[:])
             mu_logvar[n][head] = result
@@ -306,15 +337,15 @@ def tile_enhancedmlpdenoisingvae_pa_kernel(
             if not 0 <= n < TILES:
                 return
             g, t = divmod(n, PAIR_TILES)
-            z = stds[n]
-            nc.vector.tensor_tensor(out=z[:], in0=z[:], in1=noise[:, g, t, :], op=ALU.mult)
+            parts[n] = part.tile([P, L], F32, tag="part", name="part")
+            nc.gpsimd.tensor_tensor(out=parts[n][:], in0=stds[n][:], in1=noise[:, g, t, :], op=ALU.mult)
 
         def add_mu(n):
             if not 0 <= n < TILES:
                 return
             g, t = divmod(n, PAIR_TILES)
             z = stds[n]
-            nc.vector.tensor_tensor(out=z[:], in0=z[:], in1=mu_logvar[n][0][:], op=ALU.add)
+            nc.vector.tensor_tensor(out=z[:], in0=parts[n][:], in1=mu_logvar[n][0][:], op=ALU.add)
             nc.sync.dma_start(out=out_groups[2][g][:, t, :], in_=z[:])
 
         identity = consts.tile([P, P], F32)
@@ -341,14 +372,9 @@ def tile_enhancedmlpdenoisingvae_pa_kernel(
         load_weights(1)
         load_rows(1)
         load_rows(2)
+        quantise_weights(0)
         load_weights(2)
         load_rows(3)
-        load_weights(3)
-        for g in range(4, PAIRS):
-            load_rows(g)
-        for quarter in range(4):
-            load_noise(quarter)
-        quantise_weights(0)
 
         bias1 = consts.tile([P, H], F32)
         for i in range(2):
@@ -377,25 +403,38 @@ def tile_enhancedmlpdenoisingvae_pa_kernel(
                 )
                 nc.vector.tensor_copy(out=bias2[:, i * L : (i + 1) * L], in_=spread[:])
 
-        for k in range(TILES + LAG_Z):
-            for c in range(PASSES):
-                turn_hidden(k - LAG_TURN, c)
+        for k in range(TILES + LAG_ADD_MU):
+            scale_noise(k - LAG_SCALE_NOISE)
             turn_rows(k)
-            for half in range(2):
-                encode(k - LAG_ENCODE, half)
-            scale_noise(k - LAG_Z)
-            for head in (1, 0):
-                heads(k - LAG_HEADS, head)
+            multiply_first(k - LAG_ENCODE, 0)
+            turn_hidden(k - LAG_TURN, 0)
+            multiply_head(k - LAG_HEADS, 1)
+            multiply_first(k - LAG_ENCODE, 1)
+            turn_hidden(k - LAG_TURN, 1)
+            multiply_head(k - LAG_HEADS, 0)
+            add_head_bias(k - LAG_HEAD_BIAS, 1)
+            add_first_bias(k - LAG_ADD_BIAS, 0)
+            add_first_bias(k - LAG_ADD_BIAS, 1)
+            add_head_bias(k - LAG_HEAD_BIAS, 0)
+            group_rows(k)
+            gain_and_shift(k - LAG_TURN, 0)
             normalise(k - LAG_NORMALISE)
-            leaky_relu(k - LAG_TURN, 0)
-            add_mu(k - LAG_Z)
-            quantise_rows(k)
-            leaky_relu(k - LAG_TURN, 1)
-            variance(k - LAG_ENCODE)
-            exponent(k - LAG_HEADS)
+            gain_and_shift(k - LAG_TURN, 1)
+            variance(k - LAG_ADD_BIAS)
+            exponent(k - LAG_HEAD_BIAS)
             quantise_hidden(k - LAG_REQUANTISE)
+            quantise_rows(k - LAG_QUANTISE)
+            leaky_relu(k - LAG_LRELU, 0)
+            add_mu(k - LAG_ADD_MU)
+            leaky_relu(k - LAG_LRELU, 1)
             for unit in range(1, UNITS):
                 if k == UNIT_TICK[unit]:
                     quantise_weights(unit)
+            if k == UNIT_TICK[1]:
+                load_weights(3)
+                for g in range(4, PAIRS):
+                    load_rows(g)
+                for quarter in range(4):
+                    load_noise(quarter)
             if k == BIAS_TICK:
                 spread_head_biases()

@@ -28,21 +28,24 @@ TILES = B // P
 PAIR_TILES = 2
 PAIRS = TILES // PAIR_TILES
 UNITS = 4
-UNIT_TICK = {1: 0, 2: 2, 3: 6}
-BIAS_TICK = 7
-EARLY_TILES = 5
+UNIT_TICK = {1: 0, 2: 2, 3: 7}
+BIAS_TICK = 8
+
+GPSIMD_NORMALISES = [n for n in range(12) if n % 3 != 1]
+VECTOR_NORMALISES = [1]
+VECTOR_SCALES = [n for n in range(13, TILES)]
 
 LAG_QUANTISE = 1
 LAG_ENCODE = 3
 LAG_ADD_BIAS = 4
 LAG_NORMALISE = 6
-LAG_TURN = 7
-LAG_LRELU = 8
-LAG_REQUANTISE = 9
-LAG_HEADS = 10
-LAG_HEAD_BIAS = 11
-LAG_SCALE_NOISE = 12
-LAG_ADD_MU = 13
+LAG_TURN = 8
+LAG_LRELU = 9
+LAG_REQUANTISE = 10
+LAG_HEADS = 11
+LAG_HEAD_BIAS = 12
+LAG_SCALE_NOISE = 13
+LAG_ADD_MU = 14
 
 FLOPS = 2 * B * H * H + 2 * 2 * B * H * L
 
@@ -57,8 +60,8 @@ def tile_enhancedmlpdenoisingvae_pa_kernel(
         raw = stack.enter_context(tc.tile_pool(name="raw", bufs=PAIRS))
         rows = stack.enter_context(tc.tile_pool(name="rows", bufs=4))
         junk = stack.enter_context(tc.tile_pool(name="junk", bufs=2))
-        encoded = stack.enter_context(tc.tile_pool(name="encoded", bufs=6))
-        normed = stack.enter_context(tc.tile_pool(name="normed", bufs=8))
+        encoded = stack.enter_context(tc.tile_pool(name="encoded", bufs=5))
+        normed = stack.enter_context(tc.tile_pool(name="normed", bufs=6))
         small = stack.enter_context(tc.tile_pool(name="small", bufs=8))
         stage = stack.enter_context(tc.tile_pool(name="stage", bufs=4))
         results = stack.enter_context(tc.tile_pool(name="results", bufs=4))
@@ -99,7 +102,8 @@ def tile_enhancedmlpdenoisingvae_pa_kernel(
         def load_weights(unit):
             w_raw[unit] = consts.tile([P, 4, H], BF16, name="w_raw%d" % (unit % 2))
             for d in range(2):
-                nc.sync.dma_start(out=w_raw[unit][:, 2 * d : 2 * d + 2, :], in_=weight_sources[unit][d])
+                for i in range(2):
+                    nc.sync.dma_start(out=w_raw[unit][:, 2 * d + i, :], in_=weight_sources[unit][d][:, i, :])
 
         def load_rows(g):
             h1_raw[g] = raw.tile([P, PAIR_TILES, H], BF16, tag="h1_raw", name="h1_raw")
@@ -222,24 +226,32 @@ def tile_enhancedmlpdenoisingvae_pa_kernel(
             )
             rstds[n] = small.tile([P, 1], F32, tag="rstd", name="rstd")
             nc.gpsimd.tensor_tensor(out=rstds[n][:], in0=var_eps[:], in1=neg_half[:], op=ALU.pow)
-            if n >= EARLY_TILES:
+            if n not in GPSIMD_NORMALISES and n not in VECTOR_NORMALISES:
                 offsets[n] = small.tile([P, 1], F32, tag="offset", name="offset")
                 nc.gpsimd.tensor_tensor(out=offsets[n][:], in0=neg_means[n][:], in1=rstds[n][:], op=ALU.mult)
 
-        def normalise(n):
-            if not 0 <= n < TILES:
-                return
+        def normalise_on(engine, n):
             normalised[n] = normed.tile([P, H], F32, tag="y", name="y")
-            if n < EARLY_TILES:
-                nc.vector.tensor_scalar(
-                    out=normalised[n][:],
-                    in0=encodings[n][:],
-                    scalar1=neg_means[n][:],
-                    scalar2=rstds[n][:],
-                    op0=ALU.add,
-                    op1=ALU.mult,
-                )
+            engine.tensor_scalar(
+                out=normalised[n][:],
+                in0=encodings[n][:],
+                scalar1=neg_means[n][:],
+                scalar2=rstds[n][:],
+                op0=ALU.add,
+                op1=ALU.mult,
+            )
+
+        def normalise_on_gpsimd(n):
+            if n in GPSIMD_NORMALISES:
+                normalise_on(nc.gpsimd, n)
+
+        def normalise(n):
+            if not 0 <= n < TILES or n in GPSIMD_NORMALISES:
+                return
+            if n in VECTOR_NORMALISES:
+                normalise_on(nc.vector, n)
             else:
+                normalised[n] = normed.tile([P, H], F32, tag="y", name="y")
                 nc.scalar.activation(
                     out=normalised[n][:],
                     in_=encodings[n][:],
@@ -337,8 +349,13 @@ def tile_enhancedmlpdenoisingvae_pa_kernel(
             if not 0 <= n < TILES:
                 return
             g, t = divmod(n, PAIR_TILES)
-            parts[n] = part.tile([P, L], F32, tag="part", name="part")
-            nc.gpsimd.tensor_tensor(out=parts[n][:], in0=stds[n][:], in1=noise[:, g, t, :], op=ALU.mult)
+            if n in VECTOR_SCALES:
+                parts[n] = stds[n]
+                engine = nc.vector
+            else:
+                parts[n] = part.tile([P, L], F32, tag="part", name="part")
+                engine = nc.gpsimd
+            engine.tensor_tensor(out=parts[n][:], in0=stds[n][:], in1=noise[:, g, t, :], op=ALU.mult)
 
         def add_mu(n):
             if not 0 <= n < TILES:
@@ -401,32 +418,28 @@ def tile_enhancedmlpdenoisingvae_pa_kernel(
                 nc.tensor.matmul(
                     out=spread[:], lhsT=ones[:], rhs=bias_rows[:, H + i * L : H + (i + 1) * L], start=True, stop=True
                 )
-                nc.vector.tensor_copy(out=bias2[:, i * L : (i + 1) * L], in_=spread[:])
+                nc.scalar.copy(out=bias2[:, i * L : (i + 1) * L], in_=spread[:])
 
         for k in range(TILES + LAG_ADD_MU):
-            scale_noise(k - LAG_SCALE_NOISE)
             turn_rows(k)
+            multiply_head(k - LAG_HEADS, 1)
             multiply_first(k - LAG_ENCODE, 0)
             turn_hidden(k - LAG_TURN, 0)
-            multiply_head(k - LAG_HEADS, 1)
-            multiply_first(k - LAG_ENCODE, 1)
             turn_hidden(k - LAG_TURN, 1)
             multiply_head(k - LAG_HEADS, 0)
+            multiply_first(k - LAG_ENCODE, 1)
             add_head_bias(k - LAG_HEAD_BIAS, 1)
+            add_head_bias(k - LAG_HEAD_BIAS, 0)
             add_first_bias(k - LAG_ADD_BIAS, 0)
             add_first_bias(k - LAG_ADD_BIAS, 1)
-            add_head_bias(k - LAG_HEAD_BIAS, 0)
+            scale_noise(k - LAG_SCALE_NOISE)
+            normalise_on_gpsimd(k - LAG_NORMALISE - 1)
             group_rows(k)
-            gain_and_shift(k - LAG_TURN, 0)
             normalise(k - LAG_NORMALISE)
+            gain_and_shift(k - LAG_TURN, 0)
             gain_and_shift(k - LAG_TURN, 1)
             variance(k - LAG_ADD_BIAS)
             exponent(k - LAG_HEAD_BIAS)
-            quantise_hidden(k - LAG_REQUANTISE)
-            quantise_rows(k - LAG_QUANTISE)
-            leaky_relu(k - LAG_LRELU, 0)
-            add_mu(k - LAG_ADD_MU)
-            leaky_relu(k - LAG_LRELU, 1)
             for unit in range(1, UNITS):
                 if k == UNIT_TICK[unit]:
                     quantise_weights(unit)
@@ -438,3 +451,8 @@ def tile_enhancedmlpdenoisingvae_pa_kernel(
                     load_noise(quarter)
             if k == BIAS_TICK:
                 spread_head_biases()
+            quantise_rows(k - LAG_QUANTISE)
+            quantise_hidden(k - LAG_REQUANTISE)
+            leaky_relu(k - LAG_LRELU, 0)
+            add_mu(k - LAG_ADD_MU)
+            leaky_relu(k - LAG_LRELU, 1)

@@ -29,10 +29,10 @@ PAIR_TILES = 2
 PAIRS = TILES // PAIR_TILES
 UNITS = 4
 UNIT_TICK = {1: 0, 2: 2, 3: 7}
+UNIT_QUANTISE_TICK = {1: 0, 2: 3, 3: 8}
 BIAS_TICK = 8
 
-GPSIMD_NORMALISES = [n for n in range(12) if n % 3 != 1]
-VECTOR_NORMALISES = [1]
+EARLY_TILES = 5
 VECTOR_SCALES = [n for n in range(13, TILES)]
 
 LAG_QUANTISE = 1
@@ -124,22 +124,28 @@ def tile_enhancedmlpdenoisingvae_pa_kernel(
         def lay_side_by_side(turned, grouped_words, copy):
             copy(out=grouped_words, in_=turned[:].rearrange("p (c u) r -> p c r u", u=HALVES))
 
-        def quantise_weights(unit):
+        w_grouped = {}
+
+        def turn_weights(unit):
             w_words = w_raw[unit][:].bitcast(F32)
-            w_grouped = consts.tile([P, PASSES, N_TILE, PACK], BF16, name="w_grouped%d" % (unit % 2), align_bytes=64)
-            w_grouped_words = w_grouped[:].bitcast(F32)
+            w_grouped[unit] = consts.tile(
+                [P, PASSES, N_TILE, PACK], BF16, name="w_grouped%d" % (unit % 2), align_bytes=64
+            )
+            w_grouped_words = w_grouped[unit][:].bitcast(F32)
             for i in range(4):
                 lay_side_by_side(
                     turn_words(w_words[:, i, :]),
                     w_grouped_words[:, :, i * P : (i + 1) * P, :],
                     nc.vector.tensor_copy if i % 2 == 0 else nc.scalar.copy,
                 )
+
+        def quantise_weights(unit):
             w_codes[unit] = consts.tile([P, PASSES, N_TILE], U32, name="w_codes%d" % unit, align_bytes=64)
             w_scales[unit] = consts.tile([P, PASSES, N_TILE], U8, name="w_scales%d" % unit, align_bytes=64)
             nc.vector.quantize_mx(
                 out=w_codes[unit][:].rearrange("p c n -> p (c n)").bitcast(FP8X4),
                 scales=w_scales[unit][:].rearrange("p c n -> p (c n)"),
-                in_=w_grouped[:].rearrange("p c n t -> p (c n t)"),
+                in_=w_grouped[unit][:].rearrange("p c n t -> p (c n t)"),
             )
 
         turned_rows = {}
@@ -226,32 +232,24 @@ def tile_enhancedmlpdenoisingvae_pa_kernel(
             )
             rstds[n] = small.tile([P, 1], F32, tag="rstd", name="rstd")
             nc.gpsimd.tensor_tensor(out=rstds[n][:], in0=var_eps[:], in1=neg_half[:], op=ALU.pow)
-            if n not in GPSIMD_NORMALISES and n not in VECTOR_NORMALISES:
+            if n >= EARLY_TILES:
                 offsets[n] = small.tile([P, 1], F32, tag="offset", name="offset")
                 nc.gpsimd.tensor_tensor(out=offsets[n][:], in0=neg_means[n][:], in1=rstds[n][:], op=ALU.mult)
 
-        def normalise_on(engine, n):
-            normalised[n] = normed.tile([P, H], F32, tag="y", name="y")
-            engine.tensor_scalar(
-                out=normalised[n][:],
-                in0=encodings[n][:],
-                scalar1=neg_means[n][:],
-                scalar2=rstds[n][:],
-                op0=ALU.add,
-                op1=ALU.mult,
-            )
-
-        def normalise_on_gpsimd(n):
-            if n in GPSIMD_NORMALISES:
-                normalise_on(nc.gpsimd, n)
-
         def normalise(n):
-            if not 0 <= n < TILES or n in GPSIMD_NORMALISES:
+            if not 0 <= n < TILES:
                 return
-            if n in VECTOR_NORMALISES:
-                normalise_on(nc.vector, n)
+            normalised[n] = normed.tile([P, H], F32, tag="y", name="y")
+            if n < EARLY_TILES:
+                nc.vector.tensor_scalar(
+                    out=normalised[n][:],
+                    in0=encodings[n][:],
+                    scalar1=neg_means[n][:],
+                    scalar2=rstds[n][:],
+                    op0=ALU.add,
+                    op1=ALU.mult,
+                )
             else:
-                normalised[n] = normed.tile([P, H], F32, tag="y", name="y")
                 nc.scalar.activation(
                     out=normalised[n][:],
                     in_=encodings[n][:],
@@ -389,6 +387,7 @@ def tile_enhancedmlpdenoisingvae_pa_kernel(
         load_weights(1)
         load_rows(1)
         load_rows(2)
+        turn_weights(0)
         quantise_weights(0)
         load_weights(2)
         load_rows(3)
@@ -433,7 +432,6 @@ def tile_enhancedmlpdenoisingvae_pa_kernel(
             add_first_bias(k - LAG_ADD_BIAS, 0)
             add_first_bias(k - LAG_ADD_BIAS, 1)
             scale_noise(k - LAG_SCALE_NOISE)
-            normalise_on_gpsimd(k - LAG_NORMALISE - 1)
             group_rows(k)
             normalise(k - LAG_NORMALISE)
             gain_and_shift(k - LAG_TURN, 0)
@@ -442,7 +440,7 @@ def tile_enhancedmlpdenoisingvae_pa_kernel(
             exponent(k - LAG_HEAD_BIAS)
             for unit in range(1, UNITS):
                 if k == UNIT_TICK[unit]:
-                    quantise_weights(unit)
+                    turn_weights(unit)
             if k == UNIT_TICK[1]:
                 load_weights(3)
                 for g in range(4, PAIRS):
@@ -456,3 +454,6 @@ def tile_enhancedmlpdenoisingvae_pa_kernel(
             leaky_relu(k - LAG_LRELU, 0)
             add_mu(k - LAG_ADD_MU)
             leaky_relu(k - LAG_LRELU, 1)
+            for unit in range(1, UNITS):
+                if k == UNIT_QUANTISE_TICK[unit]:
+                    quantise_weights(unit)

@@ -33,7 +33,7 @@ UNIT_QUANTISE_TICK = {1: 0, 2: 3, 3: 8}
 BIAS_TICK = 8
 
 EARLY_TILES = 5
-VECTOR_SCALES = [n for n in range(13, TILES)]
+VECTOR_ADDS = [n for n in range(13, TILES)]
 
 LAG_QUANTISE = 1
 LAG_ENCODE = 3
@@ -65,7 +65,6 @@ def tile_enhancedmlpdenoisingvae_pa_kernel(
         small = stack.enter_context(tc.tile_pool(name="small", bufs=8))
         stage = stack.enter_context(tc.tile_pool(name="stage", bufs=4))
         results = stack.enter_context(tc.tile_pool(name="results", bufs=4))
-        part = stack.enter_context(tc.tile_pool(name="part", bufs=1))
         psum = stack.enter_context(tc.psum_pool(name="psum", bufs=4))
 
         w2_rows = enc_w2.rearrange("(a q e) k -> a q e k", a=4, e=PAIR)
@@ -97,7 +96,6 @@ def tile_enhancedmlpdenoisingvae_pa_kernel(
         h_scales = {}
         mu_logvar = {}
         stds = {}
-        parts = {}
 
         def load_weights(unit):
             w_raw[unit] = consts.tile([P, 4, H], BF16, name="w_raw%d" % (unit % 2))
@@ -347,20 +345,15 @@ def tile_enhancedmlpdenoisingvae_pa_kernel(
             if not 0 <= n < TILES:
                 return
             g, t = divmod(n, PAIR_TILES)
-            if n in VECTOR_SCALES:
-                parts[n] = stds[n]
-                engine = nc.vector
-            else:
-                parts[n] = part.tile([P, L], F32, tag="part", name="part")
-                engine = nc.gpsimd
-            engine.tensor_tensor(out=parts[n][:], in0=stds[n][:], in1=noise[:, g, t, :], op=ALU.mult)
+            nc.vector.tensor_tensor(out=stds[n][:], in0=stds[n][:], in1=noise[:, g, t, :], op=ALU.mult)
 
         def add_mu(n):
             if not 0 <= n < TILES:
                 return
             g, t = divmod(n, PAIR_TILES)
             z = stds[n]
-            nc.vector.tensor_tensor(out=z[:], in0=parts[n][:], in1=mu_logvar[n][0][:], op=ALU.add)
+            engine = nc.vector if n in VECTOR_ADDS else nc.gpsimd
+            engine.tensor_tensor(out=z[:], in0=z[:], in1=mu_logvar[n][0][:], op=ALU.add)
             nc.sync.dma_start(out=out_groups[2][g][:, t, :], in_=z[:])
 
         identity = consts.tile([P, P], F32)
@@ -431,7 +424,7 @@ def tile_enhancedmlpdenoisingvae_pa_kernel(
             add_head_bias(k - LAG_HEAD_BIAS, 0)
             add_first_bias(k - LAG_ADD_BIAS, 0)
             add_first_bias(k - LAG_ADD_BIAS, 1)
-            scale_noise(k - LAG_SCALE_NOISE)
+            add_mu(k - LAG_ADD_MU)
             group_rows(k)
             normalise(k - LAG_NORMALISE)
             gain_and_shift(k - LAG_TURN, 0)
@@ -452,8 +445,8 @@ def tile_enhancedmlpdenoisingvae_pa_kernel(
             quantise_rows(k - LAG_QUANTISE)
             quantise_hidden(k - LAG_REQUANTISE)
             leaky_relu(k - LAG_LRELU, 0)
-            add_mu(k - LAG_ADD_MU)
             leaky_relu(k - LAG_LRELU, 1)
+            scale_noise(k - LAG_SCALE_NOISE)
             for unit in range(1, UNITS):
                 if k == UNIT_QUANTISE_TICK[unit]:
                     quantise_weights(unit)

@@ -33,7 +33,7 @@ UNIT_QUANTISE_TICK = {1: 0, 2: 3, 3: 8}
 BIAS_TICK = 8
 
 EARLY_TILES = 5
-VECTOR_ADDS = [n for n in range(13, TILES)]
+VECTOR_ADDS = [6, 13, 14, 15]
 
 LAG_QUANTISE = 1
 LAG_ENCODE = 3
@@ -414,23 +414,22 @@ def tile_enhancedmlpdenoisingvae_pa_kernel(
 
         for k in range(TILES + LAG_ADD_MU):
             turn_rows(k)
-            multiply_head(k - LAG_HEADS, 1)
-            multiply_first(k - LAG_ENCODE, 0)
             turn_hidden(k - LAG_TURN, 0)
-            turn_hidden(k - LAG_TURN, 1)
+            multiply_head(k - LAG_HEADS, 1)
             multiply_head(k - LAG_HEADS, 0)
-            multiply_first(k - LAG_ENCODE, 1)
+            turn_hidden(k - LAG_TURN, 1)
             add_head_bias(k - LAG_HEAD_BIAS, 1)
             add_head_bias(k - LAG_HEAD_BIAS, 0)
             add_first_bias(k - LAG_ADD_BIAS, 0)
             add_first_bias(k - LAG_ADD_BIAS, 1)
             add_mu(k - LAG_ADD_MU)
             group_rows(k)
-            normalise(k - LAG_NORMALISE)
             gain_and_shift(k - LAG_TURN, 0)
             gain_and_shift(k - LAG_TURN, 1)
-            variance(k - LAG_ADD_BIAS)
-            exponent(k - LAG_HEAD_BIAS)
+            leaky_relu(k - LAG_LRELU, 0)
+            quantise_hidden(k - LAG_REQUANTISE)
+            scale_noise(k - LAG_SCALE_NOISE)
+            quantise_rows(k - LAG_QUANTISE)
             for unit in range(1, UNITS):
                 if k == UNIT_TICK[unit]:
                     turn_weights(unit)
@@ -442,11 +441,12 @@ def tile_enhancedmlpdenoisingvae_pa_kernel(
                     load_noise(quarter)
             if k == BIAS_TICK:
                 spread_head_biases()
-            quantise_rows(k - LAG_QUANTISE)
-            quantise_hidden(k - LAG_REQUANTISE)
-            leaky_relu(k - LAG_LRELU, 0)
-            leaky_relu(k - LAG_LRELU, 1)
-            scale_noise(k - LAG_SCALE_NOISE)
             for unit in range(1, UNITS):
                 if k == UNIT_QUANTISE_TICK[unit]:
                     quantise_weights(unit)
+            multiply_first(k - LAG_ENCODE, 0)
+            multiply_first(k - LAG_ENCODE, 1)
+            exponent(k - LAG_HEAD_BIAS)
+            variance(k - LAG_ADD_BIAS)
+            normalise(k - LAG_NORMALISE)
+            leaky_relu(k - LAG_LRELU, 1)

from contextlib import ExitStack

import concourse.mybir as mybir
from concourse.masks import make_identity

F32 = mybir.dt.float32
BF16 = mybir.dt.bfloat16
U32 = mybir.dt.uint32
U8 = mybir.dt.uint8
FP8X4 = mybir.dt.float8_e4m3fn_x4
ALU = mybir.AluOpType
ACT = mybir.ActivationFunctionType

B, H, L = 2048, 1024, 512
LN_EPS = 1e-5
SLOPE = 0.2

P = 128
PACK = 4
PAIR = 2
LINE = 4
HALVES = PACK // PAIR
K_PASS = P * PACK
PASSES = H // K_PASS
N_TILE = 512
BLOCKS = H // P
TILES = B // P
PAIR_TILES = 2
PAIRS = TILES // PAIR_TILES
UNITS = 4
UNIT_TICK = {1: 0, 2: 2, 3: 7}
UNIT_QUANTISE_TICK = {1: 0, 2: 3, 3: 8}
BIAS_TICK = 8

EARLY_TILES = 5
VECTOR_ADDS = [6, 13, 14, 15]

LAG_QUANTISE = 1
LAG_ENCODE = 3
LAG_ADD_BIAS = 4
LAG_NORMALISE = 6
LAG_TURN = 8
LAG_LRELU = 9
LAG_REQUANTISE = 10
LAG_HEADS = 11
LAG_HEAD_BIAS = 12
LAG_SCALE_NOISE = 13
LAG_ADD_MU = 14

FLOPS = 2 * B * H * H + 2 * 2 * B * H * L


def tile_enhancedmlpdenoisingvae_pa_kernel(
    tc, h1, eps, enc_w2, enc_b2, ln2_g, ln2_b, mu_w, mu_b, lv_w, lv_b, out_0, out_1, out_2
):
    nc = tc.nc
    with ExitStack() as stack:
        stack.enter_context(tc.manual_schedule())
        consts = stack.enter_context(tc.tile_pool(name="consts", bufs=1))
        raw = stack.enter_context(tc.tile_pool(name="raw", bufs=PAIRS))
        rows = stack.enter_context(tc.tile_pool(name="rows", bufs=4))
        junk = stack.enter_context(tc.tile_pool(name="junk", bufs=2))
        encoded = stack.enter_context(tc.tile_pool(name="encoded", bufs=5))
        normed = stack.enter_context(tc.tile_pool(name="normed", bufs=6))
        small = stack.enter_context(tc.tile_pool(name="small", bufs=8))
        stage = stack.enter_context(tc.tile_pool(name="stage", bufs=4))
        results = stack.enter_context(tc.tile_pool(name="results", bufs=4))
        psum = stack.enter_context(tc.psum_pool(name="psum", bufs=4))

        w2_rows = enc_w2.rearrange("(a q e) k -> a q e k", a=4, e=PAIR)
        mu_rows = mu_w.rearrange("(d i r) k -> d r i k", d=2, i=2)
        lv_rows = lv_w.rearrange("(d i r) k -> d r i k", d=2, i=2)
        weight_sources = [w2_rows[0:2], w2_rows[2:4], mu_rows, lv_rows]
        h1_groups = h1.rearrange("(g p t) k -> g p (t k)", p=P, t=PAIR_TILES)
        eps_rows = eps.rearrange("(g p t) l -> p g (t l)", p=P, t=PAIR_TILES)
        out_groups = [
            o.rearrange("(g p t) l -> g p t l", p=P, t=PAIR_TILES) for o in (out_0, out_1, out_2)
        ]

        w_raw = {}
        w_codes = {}
        w_scales = {}
        h1_raw = {}
        h1_grouped = {}
        h1_codes = {}
        h1_scales = {}
        encodings = {}
        row_sums = {}
        neg_means = {}
        rstds = {}
        offsets = {}
        normalised = {}
        affine = {}
        h_grouped = {}
        h_codes = {}
        h_scales = {}
        mu_logvar = {}
        stds = {}

        def load_weights(unit):
            w_raw[unit] = consts.tile([P, 4, H], BF16, name="w_raw%d" % (unit % 2))
            for d in range(2):
                for i in range(2):
                    nc.sync.dma_start(out=w_raw[unit][:, 2 * d + i, :], in_=weight_sources[unit][d][:, i, :])

        def load_rows(g):
            h1_raw[g] = raw.tile([P, PAIR_TILES, H], BF16, tag="h1_raw", name="h1_raw")
            nc.sync.dma_start(out=h1_raw[g][:].rearrange("p t k -> p (t k)"), in_=h1_groups[g])

        def load_noise(quarter):
            groups = slice(quarter * 2, quarter * 2 + 2)
            nc.sync.dma_start(
                out=noise[:, groups, :, :].rearrange("p g t l -> p g (t l)"), in_=eps_rows[:, groups, :]
            )

        def turn_words(row_words):
            turned = psum.tile([P, PASSES * HALVES, P], F32, tag="turned", name="turned")
            for w in range(PASSES * HALVES):
                nc.tensor.transpose(turned[:, w, :], row_words[:, w * P : (w + 1) * P], identity[:])
            return turned

        def lay_side_by_side(turned, grouped_words, copy):
            copy(out=grouped_words, in_=turned[:].rearrange("p (c u) r -> p c r u", u=HALVES))

        w_grouped = {}

        def turn_weights(unit):
            w_words = w_raw[unit][:].bitcast(F32)
            w_grouped[unit] = consts.tile(
                [P, PASSES, N_TILE, PACK], BF16, name="w_grouped%d" % (unit % 2), align_bytes=64
            )
            w_grouped_words = w_grouped[unit][:].bitcast(F32)
            for i in range(4):
                lay_side_by_side(
                    turn_words(w_words[:, i, :]),
                    w_grouped_words[:, :, i * P : (i + 1) * P, :],
                    nc.vector.tensor_copy if i % 2 == 0 else nc.scalar.copy,
                )

        def quantise_weights(unit):
            w_codes[unit] = consts.tile([P, PASSES, N_TILE], U32, name="w_codes%d" % unit, align_bytes=64)
            w_scales[unit] = consts.tile([P, PASSES, N_TILE], U8, name="w_scales%d" % unit, align_bytes=64)
            nc.vector.quantize_mx(
                out=w_codes[unit][:].rearrange("p c n -> p (c n)").bitcast(FP8X4),
                scales=w_scales[unit][:].rearrange("p c n -> p (c n)"),
                in_=w_grouped[unit][:].rearrange("p c n t -> p (c n t)"),
            )

        turned_rows = {}

        def turn_rows(n):
            if not 0 <= n < TILES:
                return
            g, t = divmod(n, PAIR_TILES)
            turned_rows[n] = turn_words(h1_raw[g][:].bitcast(F32)[:, t, :])

        def group_rows(n):
            if not 0 <= n < TILES:
                return
            h1_grouped[n] = rows.tile([P, PASSES, P, PACK], BF16, tag="h1_grouped", name="h1_grouped", align_bytes=64)
            lay_side_by_side(turned_rows[n], h1_grouped[n][:].bitcast(F32), nc.scalar.copy)

        def quantise_rows(n):
            if not 0 <= n < TILES:
                return
            h1_codes[n] = rows.tile([P, PASSES, P], U32, tag="h1_codes", name="h1_codes", align_bytes=64)
            h1_scales[n] = rows.tile([P, PASSES, P], U8, tag="h1_scales", name="h1_scales", align_bytes=64)
            nc.vector.quantize_mx(
                out=h1_codes[n][:].rearrange("p c r -> p (c r)").bitcast(FP8X4),
                scales=h1_scales[n][:].rearrange("p c r -> p (c r)"),
                in_=h1_grouped[n][:].rearrange("p c r t -> p (c r t)"),
            )

        accs = {}

        def multiply_first(n, half):
            if not 0 <= n < TILES:
                return
            acc = psum.tile([P, N_TILE], F32, tag="acc", name="acc")
            accs[n, half] = acc
            for c in range(PASSES):
                nc.tensor.matmul_mx(
                    out=acc[:],
                    lhsT=h1_codes[n][:, c, :].bitcast(FP8X4),
                    lhsT_scale=h1_scales[n][:, c, :],
                    rhs=w_codes[half][:, c, :].bitcast(FP8X4),
                    rhs_scale=w_scales[half][:, c, :],
                    start=(c == 0),
                    stop=(c == PASSES - 1),
                )

        def add_first_bias(n, half):
            if not 0 <= n < TILES:
                return
            if half == 0:
                encodings[n] = encoded.tile([P, H], F32, tag="x", name="x")
                row_sums[n] = small.tile([P, 2], F32, tag="row_sums", name="row_sums")
            cols = slice(half * N_TILE, (half + 1) * N_TILE)
            nc.vector.scalar_tensor_tensor(
                out=encodings[n][:, cols],
                in0=accs[n, half][:],
                scalar=1.0,
                in1=bias1[:, cols],
                op0=ALU.mult,
                op1=ALU.add,
                accum_out=row_sums[n][:, half : half + 1],
            )

        def variance(n):
            if not 0 <= n < TILES:
                return
            shares = small.tile([P, 2], F32, tag="shares")
            neg_means[n] = small.tile([P, 1], F32, tag="neg_mean", name="neg_mean")
            nc.scalar.activation(
                out=shares[:], in_=row_sums[n][:], func=ACT.Identity, scale=-1.0 / H, accum_out=neg_means[n][:]
            )
            squares = junk.tile([P, H], BF16, tag="squares")
            sum_sq = small.tile([P, 1], F32, tag="sum_sq")
            nc.scalar.activation(
                out=squares[:],
                in_=encodings[n][:],
                func=ACT.Square,
                bias=neg_means[n][:],
                scale=1.0,
                accum_out=sum_sq[:],
            )
            var_eps = small.tile([P, 1], F32, tag="var_eps")
            nc.gpsimd.tensor_scalar(
                out=var_eps[:], in0=sum_sq[:], scalar1=1.0 / H, scalar2=LN_EPS, op0=ALU.mult, op1=ALU.add
            )
            rstds[n] = small.tile([P, 1], F32, tag="rstd", name="rstd")
            nc.gpsimd.tensor_tensor(out=rstds[n][:], in0=var_eps[:], in1=neg_half[:], op=ALU.pow)
            if n >= EARLY_TILES:
                offsets[n] = small.tile([P, 1], F32, tag="offset", name="offset")
                nc.gpsimd.tensor_tensor(out=offsets[n][:], in0=neg_means[n][:], in1=rstds[n][:], op=ALU.mult)

        def normalise(n):
            if not 0 <= n < TILES:
                return
            normalised[n] = normed.tile([P, H], F32, tag="y", name="y")
            if n < EARLY_TILES:
                nc.vector.tensor_scalar(
                    out=normalised[n][:],
                    in0=encodings[n][:],
                    scalar1=neg_means[n][:],
                    scalar2=rstds[n][:],
                    op0=ALU.add,
                    op1=ALU.mult,
                )
            else:
                nc.scalar.activation(
                    out=normalised[n][:],
                    in_=encodings[n][:],
                    func=ACT.Identity,
                    bias=offsets[n][:],
                    scale=rstds[n][:],
                )

        turned_hidden = {}

        def turn_hidden(n, c):
            if not 0 <= n < TILES:
                return
            turned_y = psum.tile([P, PACK, P], F32, tag="turned", name="turned")
            turned_hidden[n, c] = turned_y
            for t in range(PACK):
                j = c * PACK + t
                nc.tensor.transpose(turned_y[:, t, :], normalised[n][:, j * P : (j + 1) * P], identity[:])

        def gain_and_shift(n, c):
            if not 0 <= n < TILES:
                return
            affine[n, c] = stage.tile([P, P // LINE, PACK, LINE], F32, tag="affine", name="affine", align_bytes=64)
            for t in range(PACK):
                j = c * PACK + t
                nc.scalar.activation(
                    out=affine[n, c][:, :, t, :],
                    in_=turned_hidden[n, c][:, t, :].rearrange("p (i a) -> p a i", i=LINE),
                    func=ACT.Identity,
                    bias=gain_shift[:, BLOCKS + j : BLOCKS + j + 1],
                    scale=gain_shift[:, j : j + 1],
                )

        def leaky_relu(n, c):
            if not 0 <= n < TILES:
                return
            if c == 0:
                h_grouped[n] = stage.tile([P, PASSES, P * PACK], BF16, tag="h_grouped", name="h_grouped", align_bytes=64)
            as_it_lies = affine[n, c][:].rearrange("p a t i -> p (a t) i")
            nc.vector.scalar_tensor_tensor(
                out=h_grouped[n][:, c, :].rearrange("p (i m) -> p m i", i=LINE),
                in0=as_it_lies,
                scalar=SLOPE,
                in1=as_it_lies,
                op0=ALU.mult,
                op1=ALU.max,
            )

        def quantise_hidden(n):
            if not 0 <= n < TILES:
                return
            h_codes[n] = stage.tile([P, PASSES, P], U32, tag="h_codes", name="h_codes", align_bytes=64)
            h_scales[n] = stage.tile([P, PASSES, P], U8, tag="h_scales", name="h_scales", align_bytes=64)
            nc.vector.quantize_mx(
                out=h_codes[n][:].rearrange("p c r -> p (c r)").bitcast(FP8X4),
                scales=h_scales[n][:].rearrange("p c r -> p (c r)"),
                in_=h_grouped[n][:].rearrange("p c m -> p (c m)"),
            )

        def multiply_head(n, head):
            if not 0 <= n < TILES:
                return
            acc = psum.tile([P, L], F32, tag="acc", name="acc")
            accs[n, 2 + head] = acc
            for c in range(PASSES):
                nc.tensor.matmul_mx(
                    out=acc[:],
                    lhsT=h_codes[n][:, c, :].bitcast(FP8X4),
                    lhsT_scale=h_scales[n][:, c, :],
                    rhs=w_codes[2 + head][:, c, :].bitcast(FP8X4),
                    rhs_scale=w_scales[2 + head][:, c, :],
                    start=(c == 0),
                    stop=(c == PASSES - 1),
                )

        def add_head_bias(n, head):
            if not 0 <= n < TILES:
                return
            g, t = divmod(n, PAIR_TILES)
            mu_logvar.setdefault(n, {})
            result = results.tile([P, L], F32, tag="head%d" % head, name="head%d" % head)
            nc.vector.tensor_tensor(
                out=result[:], in0=accs[n, 2 + head][:], in1=bias2[:, head * L : (head + 1) * L], op=ALU.add
            )
            nc.sync.dma_start(out=out_groups[head][g][:, t, :], in_=result[:])
            mu_logvar[n][head] = result

        def exponent(n):
            if not 0 <= n < TILES:
                return
            stds[n] = results.tile([P, L], F32, tag="z", name="z")
            nc.scalar.activation(out=stds[n][:], in_=mu_logvar[n][1][:], func=ACT.Exp, scale=0.5)

        def scale_noise(n):
            if not 0 <= n < TILES:
                return
            g, t = divmod(n, PAIR_TILES)
            nc.vector.tensor_tensor(out=stds[n][:], in0=stds[n][:], in1=noise[:, g, t, :], op=ALU.mult)

        def add_mu(n):
            if not 0 <= n < TILES:
                return
            g, t = divmod(n, PAIR_TILES)
            z = stds[n]
            engine = nc.vector if n in VECTOR_ADDS else nc.gpsimd
            engine.tensor_tensor(out=z[:], in0=z[:], in1=mu_logvar[n][0][:], op=ALU.add)
            nc.sync.dma_start(out=out_groups[2][g][:, t, :], in_=z[:])

        identity = consts.tile([P, P], F32)
        make_identity(nc, identity[:])
        ones = consts.tile([P, P], BF16)
        nc.vector.memset(ones[:], 1.0)
        neg_half = consts.tile([P, 1], F32)
        nc.vector.memset(neg_half[:], -0.5)
        warm = consts.tile([P, 1], F32)
        nc.scalar.activation(out=warm[:], in_=neg_half[:], func=ACT.Exp)
        bias_rows = consts.tile([P, H + 2 * L], BF16)
        nc.vector.memset(bias_rows[:], 0.0)
        nc.scalar.dma_start(out=bias_rows[0:1, 0:H], in_=enc_b2.unsqueeze(0))
        nc.scalar.dma_start(out=bias_rows[0:1, H : H + L], in_=mu_b.unsqueeze(0))
        nc.scalar.dma_start(out=bias_rows[0:1, H + L : H + 2 * L], in_=lv_b.unsqueeze(0))
        gain_rows = consts.tile([P, PAIR * P], BF16)
        nc.vector.memset(gain_rows[:], 0.0)
        nc.scalar.dma_start(out=gain_rows[0:4, :], in_=ln2_g.rearrange("(a q) -> a q", a=4))
        nc.scalar.dma_start(out=gain_rows[4:8, :], in_=ln2_b.rearrange("(a q) -> a q", a=4))

        noise = consts.tile([P, PAIRS, PAIR_TILES, L], BF16)
        load_weights(0)
        load_rows(0)
        load_weights(1)
        load_rows(1)
        load_rows(2)
        turn_weights(0)
        quantise_weights(0)
        load_weights(2)
        load_rows(3)

        bias1 = consts.tile([P, H], F32)
        for i in range(2):
            spread = psum.tile([P, N_TILE], F32, tag="acc")
            nc.tensor.matmul(
                out=spread[:], lhsT=ones[:], rhs=bias_rows[:, i * N_TILE : (i + 1) * N_TILE], start=True, stop=True
            )
            nc.scalar.copy(
                out=bias1[:, i * N_TILE : (i + 1) * N_TILE].rearrange("p (u e q) -> p u e q", u=2, e=PAIR),
                in_=spread[:].rearrange("p (u q e) -> p u e q", u=2, e=PAIR),
            )
        turned_gain = psum.tile([P, PASSES * HALVES, P], F32, tag="turned")
        nc.tensor.transpose(turned_gain[:, 0, :], gain_rows[:].bitcast(F32), identity[:])
        gain_words = consts.tile([P, BLOCKS], F32)
        nc.vector.tensor_copy(out=gain_words[:], in_=turned_gain[:, 0, 0:BLOCKS])
        gain_shift = consts.tile([P, 2 * BLOCKS], F32)
        nc.vector.tensor_copy(out=gain_shift[:], in_=gain_words[:].bitcast(BF16))

        bias2 = consts.tile([P, 2 * L], F32)

        def spread_head_biases():
            for i in range(2):
                spread = psum.tile([P, N_TILE], F32, tag="acc")
                nc.tensor.matmul(
                    out=spread[:], lhsT=ones[:], rhs=bias_rows[:, H + i * L : H + (i + 1) * L], start=True, stop=True
                )
                nc.scalar.copy(out=bias2[:, i * L : (i + 1) * L], in_=spread[:])

        for k in range(TILES + LAG_ADD_MU):
            turn_rows(k)
            turn_hidden(k - LAG_TURN, 0)
            multiply_head(k - LAG_HEADS, 1)
            multiply_head(k - LAG_HEADS, 0)
            turn_hidden(k - LAG_TURN, 1)
            add_head_bias(k - LAG_HEAD_BIAS, 1)
            add_head_bias(k - LAG_HEAD_BIAS, 0)
            add_first_bias(k - LAG_ADD_BIAS, 0)
            add_first_bias(k - LAG_ADD_BIAS, 1)
            add_mu(k - LAG_ADD_MU)
            group_rows(k)
            gain_and_shift(k - LAG_TURN, 0)
            gain_and_shift(k - LAG_TURN, 1)
            leaky_relu(k - LAG_LRELU, 0)
            quantise_hidden(k - LAG_REQUANTISE)
            scale_noise(k - LAG_SCALE_NOISE)
            quantise_rows(k - LAG_QUANTISE)
            for unit in range(1, UNITS):
                if k == UNIT_TICK[unit]:
                    turn_weights(unit)
            if k == UNIT_TICK[1]:
                load_weights(3)
                for g in range(4, PAIRS):
                    load_rows(g)
                for quarter in range(4):
                    load_noise(quarter)
            if k == BIAS_TICK:
                spread_head_biases()
            for unit in range(1, UNITS):
                if k == UNIT_QUANTISE_TICK[unit]:
                    quantise_weights(unit)
            multiply_first(k - LAG_ENCODE, 0)
            multiply_first(k - LAG_ENCODE, 1)
            exponent(k - LAG_HEAD_BIAS)
            variance(k - LAG_ADD_BIAS)
            normalise(k - LAG_NORMALISE)
            leaky_relu(k - LAG_LRELU, 1)
